import numpy as np
import ml_dtypes


def mxq(x, axis, fmt="e4m3"):
    dtype, down = {"e4m3": (ml_dtypes.float8_e4m3fn, 7), "e5m2": (ml_dtypes.float8_e5m2, 14)}[fmt]
    v = np.moveaxis(np.asarray(x, np.float32).astype(ml_dtypes.bfloat16).astype(np.float64), axis, -1)
    blocks = v.reshape(v.shape[:-1] + (-1, 32))
    amax = np.abs(blocks).max(-1, keepdims=True)
    byte = np.maximum(np.where(amax > 0, np.frexp(amax)[1] - 1 + 127, 0) - down, 1)
    scale = np.exp2(byte - 127.0)
    codes = (blocks / scale).astype(np.float32).astype(dtype).astype(np.float64)
    return np.moveaxis((codes * scale).reshape(v.shape), -1, axis)


WIDE = False


def mx_kscale(k):
    if not WIDE:
        return np.ones(k)
    levels = np.array([10, -10, 5, -5, 0])
    if k % 512:
        return np.exp2(np.random.permutation(np.resize(levels, k // 32))).repeat(32)
    a = np.empty((k // 512, 16))
    for p in range(k // 512):
        a[p, :8] = np.random.permutation(np.resize(levels, 8))
        for g in range(8):
            far = levels[np.abs(levels - a[p, g]) >= 10]
            a[p, g + 8] = far[np.random.randint(len(far))]
    return np.exp2(a.ravel()).repeat(32)


BF16 = ml_dtypes.bfloat16


def bf(x):
    return np.asarray(x, np.float32).astype(BF16)


def f64(x):
    return np.asarray(x).astype(np.float64)


N, C, D, H, W, NHEADS, KSIZE = 2, 512, 256, 32, 32, 8, 5
PAD = KSIZE // 2
HD = D // NHEADS
WIN = KSIZE * KSIZE


def _patches(t):
    tp = np.pad(t, ((0, 0), (0, 0), (PAD, PAD), (PAD, PAD)))
    return np.stack([tp[:, :, i:i + H, j:j + W] for i in range(KSIZE) for j in range(KSIZE)], axis=2)


def setup_inputs():
    s = mx_kscale(C)
    a = np.sqrt(1.5) / HD ** 0.25
    g = np.concatenate([np.full(2 * D, a), np.ones(D)])
    return {"x": bf(np.random.standard_normal((N, C, H, W)) * s[None, :, None, None]),
            "w_qkv": bf(np.random.standard_normal((3 * D, C)) * g[:, None] / np.sqrt(C) / s[None, :])}


def reference(x, w_qkv):
    xq = mxq(f64(x).reshape(N, C, H * W), 1, "e4m3")
    wq = mxq(f64(w_qkv), 1, "e4m3")
    qkv = (wq @ xq).reshape(N, 3 * D, H, W)
    Q, K, V = np.split(qkv, 3, axis=1)
    Qh = Q.reshape(N, NHEADS, HD, 1, H, W)
    scores = np.sum(_patches(K).reshape(N, NHEADS, HD, WIN, H, W) * Qh, axis=2, keepdims=True)
    e = np.exp(scores - scores.max(axis=3, keepdims=True))
    att = e / e.sum(axis=3, keepdims=True)
    out = np.sum(_patches(V).reshape(N, NHEADS, HD, WIN, H, W) * att, axis=3).reshape(N, D, H, W)
    return out

@@ -1,0 +1,598 @@
+from contextlib import ExitStack
+
+import concourse.mybir as mybir
+from concourse.masks import make_identity
+
+F32 = mybir.dt.float32
+BF16 = mybir.dt.bfloat16
+U32 = mybir.dt.uint32
+I32 = mybir.dt.int32
+U8 = mybir.dt.uint8
+FP8X4 = mybir.dt.float8_e4m3fn_x4
+ALU = mybir.AluOpType
+ACT = mybir.ActivationFunctionType
+AX = mybir.AxisListType
+
+P = 128
+FLOPS = 2 * 768 * 512 * 2048 + 2 * 2 * 2048 * 8 * 25 * 32
+
+N_CHUNKS = 25
+GROUPS = ((0, 0, 1), (0, 1, 1), (0, 2, 2), (1, 0, 4), (2, 0, 4), (3, 0, 4))
+VECTOR_REDUCED = (1, 3, 6, 12, 18, 23, 24)
+EVACUATIONS = (("v0", "v1"), ("v2", "v3"), ("v4", "k5"), ("k6", "k7"), ("v5", "v6", "v7"))
+WARMERS = 0
+FOLD_TWICE = ()
+VECTOR_OFFSETS = 13
+VECTOR_MULT = 0
+SCALAR_BUDGET = 10
+TMP_BUFS = 3
+FOLD_EVERY = 99
+EARLY_OFFSETS = 0
+K_DEAD_LAG = 0
+K_ROWS_REUSED = 2
+
+
+def tile_relation_kernel(tc, x, w_qkv, out):
+    nc = tc.nc
+    with ExitStack() as ctx:
+        ctx.enter_context(tc.manual_schedule())
+        keep = ctx.enter_context(tc.tile_pool(name="keep", bufs=1))
+        ring = ctx.enter_context(tc.tile_pool(name="ring", bufs=5))
+        soft = ctx.enter_context(tc.tile_pool(name="soft", bufs=2))
+        psum = ctx.enter_context(tc.psum_pool(name="psum", bufs=2))
+
+        ident_f = keep.tile([P, P], F32, name="ident_f")
+        make_identity(nc, ident_f[:])
+        wc = keep.tile([P, 768], U32, name="wc", align_bytes=64)
+        ws = keep.tile([P, 768], U8, name="ws", align_bytes=64)
+        k_rows = [keep.tile([P, 32, 64], F32, name="k%d" % r) for r in range(8)]
+        v_rows = [keep.tile([P, 8, 8, 32], F32, name="v%d" % r) for r in range(8)]
+        core_c = [keep.tile([P, 512], U32, name="cc%d" % r, align_bytes=64) for r in range(4)]
+        core_s = [keep.tile([P, 512], U8, name="cs%d" % r, align_bytes=64) for r in range(4)]
+
+        bank_bufs = {"w": 3, "qp": 3, "st": 2}
+
+        def bank(shape, dtype, name, tag):
+            return psum.tile(shape, dtype, name=name, tag=tag, bufs=bank_bufs[tag])
+
+        def ring_tile(shape, dtype, name):
+            return ring.tile(shape, dtype, name=name, tag="b8", align_bytes=64)
+
+        def project(dst, codes, scales, lo, hi):
+            nc.tensor.matmul_mx(
+                out=dst,
+                lhsT=codes.bitcast(FP8X4),
+                lhsT_scale=scales,
+                rhs=wc[:, lo:hi].bitcast(FP8X4),
+                rhs_scale=ws[:, lo:hi],
+                start=True,
+                stop=True,
+            )
+
+        wraw = ring_tile([P, 6, 512], BF16, "wraw")
+        nc.sync.dma_start(out=wraw[:], in_=w_qkv.rearrange("(r p) k -> p r k", p=P))
+        raws = []
+        for n in range(2):
+            raw = ring_tile([P, 4, 1024], BF16, "raw%d" % n)
+            nc.sync.dma_start(out=raw[:], in_=x[n].rearrange("(p t) h w -> p t (h w)", t=4))
+            raws.append(raw)
+
+        wgrp = ring_tile([P, 768, 4], BF16, "wgrp")
+        wgrp_f = wgrp[:].rearrange("p w t -> p (w t)").bitcast(F32).rearrange("p (w u) -> p w u", u=2)
+        for r in range(6):
+            ty, hh = divmod(r, 2)
+            words = wraw[:, r, :].bitcast(F32)
+            wt = bank([P, 2, P], F32, "wt", "w")
+            for u in range(2):
+                nc.tensor.transpose(wt[:, u, :], words[:, u:256:2], ident_f[:])
+            if ty < 2:
+                dst = wgrp_f[:, 256 * ty : 256 * (ty + 1), :].rearrange("p (c h) u -> p c h u", h=8)
+                dst = dst[:, :, 4 * hh : 4 * (hh + 1), :]
+                src = wt[:].rearrange("p u (h c) -> p c h u", c=32)
+            else:
+                dst = wgrp_f[:, 512 + P * hh : 512 + P * (hh + 1), :]
+                src = wt[:].rearrange("p u r -> p r u")
+            if r % 2 == 0:
+                nc.vector.tensor_copy(out=dst, in_=src)
+            else:
+                nc.scalar.copy(out=dst, in_=src)
+
+        inters = []
+        for n in range(2):
+            inter = ring_tile([P, 1024, 4], BF16, "inter%d" % n)
+            for eng, lo, hi in ((nc.vector.tensor_copy, 0, 640), (nc.scalar.copy, 640, 1024)):
+                eng(
+                    out=inter[:, lo:hi, :].rearrange("p (c i) t -> p c t i", i=4),
+                    in_=raws[n][:, :, lo:hi].rearrange("p t (c i) -> p c t i", i=4),
+                )
+            inters.append(
+                inter[:]
+                .rearrange("p x t -> p (x t)")
+                .bitcast(F32)
+                .rearrange("p (hb hl wb wl u) -> p hb hl wb wl u", hb=8, hl=4, wb=8, wl=4)
+            )
+            if n == 0:
+                for ty in range(3):
+                    cols = slice(256 * ty, 256 * (ty + 1))
+                    nc.vector.quantize_mx(
+                        out=wc[:, cols].bitcast(FP8X4),
+                        scales=ws[:, cols],
+                        in_=wgrp[:, cols, :].rearrange("p w t -> p (w t)"),
+                    )
+
+        tiles = {}
+        row_parts = {}
+
+        def gather_row(a):
+            grp = ring_tile([P, 4096], BF16, "grp")
+            g_f = grp[:].bitcast(F32).rearrange("p (b n hb wb u) -> p b n hb wb u", b=8, n=2, hb=8, wb=8)
+            nc.vector.memset(g_f[:, 0:2, :, :, 0, :], 0.0)
+            nc.vector.memset(g_f[:, 6:8, :, :, 7, :], 0.0)
+            for n in range(2):
+                for bs, wls, wd, wsrc in (
+                    (slice(0, 2), slice(2, 4), slice(1, 8), slice(0, 7)),
+                    (slice(2, 6), slice(0, 4), slice(0, 8), slice(0, 8)),
+                    (slice(6, 8), slice(0, 2), slice(0, 7), slice(1, 8)),
+                ):
+                    nc.vector.tensor_copy(
+                        out=g_f[:, bs, n, :, wd, :],
+                        in_=inters[n][:, :, a - 2, wsrc, wls, :].rearrange("p hb wb wl u -> p wl hb wb u"),
+                    )
+            return grp
+
+        def name_tiles(a, parts):
+            row_parts[a] = parts
+            for b0, b1, c_ap, s_ap in parts:
+                for b in range(b0, b1):
+                    cols = slice(P * (b - b0), P * (b - b0 + 1))
+                    tiles[(a, b)] = (c_ap[:, cols], s_ap[:, cols])
+
+        def quantise_row(codes, a, grp):
+            hc = codes.tile([P, 512], U32, name="hc%d" % a, align_bytes=64)
+            hs = codes.tile([P, 512], U8, name="hs%d" % a, align_bytes=64)
+            parts = (
+                (0, 2, hc[:, 0:256], hs[:, 0:256]),
+                (2, 6, core_c[a - 2][:], core_s[a - 2][:]),
+                (6, 8, hc[:, 256:512], hs[:, 256:512]),
+            )
+            for b0, b1, c_ap, s_ap in parts:
+                nc.vector.quantize_mx(out=c_ap.bitcast(FP8X4), scales=s_ap, in_=grp[:, 512 * b0 : 512 * b1])
+            name_tiles(a, parts)
+
+        def move_row(codes, a):
+            hc = codes.tile([P, 1024], U32, name="hc%d" % a, align_bytes=64)
+            hs = codes.tile([P, 1024], U8, name="hs%d" % a, align_bytes=64)
+            for which, dst_t, width, sh in ((2, hc, 64, 8), (3, hs, 16, 2)):
+                dst = dst_t[:].bitcast(I32).rearrange("p (m x) -> p m x", x=width)
+                nc.vector.memset(dst[:, :, 0:sh] if a < 2 else dst[:, :, width - sh : width], 0)
+                for part in row_parts[a + 4 if a < 2 else a - 4]:
+                    src = part[which].bitcast(I32).rearrange("p (m x) -> p m x", x=width)
+                    rows = slice(2 * part[0], 2 * part[1])
+                    if a < 2:
+                        nc.vector.tensor_copy(out=dst[:, rows, sh:width], in_=src[:, :, 0 : width - sh])
+                    else:
+                        nc.vector.tensor_copy(out=dst[:, rows, 0 : width - sh], in_=src[:, :, sh:width])
+            name_tiles(a, ((0, 8, hc[:], hs[:]),))
+
+        def evacuate(what, a, tags):
+            for r, b0 in enumerate((0, 2, 4, 6)):
+                ps = bank([P, 2, 256], F32, "ps", tags[r % len(tags)])
+                for u in range(2):
+                    lo = 256 if what == "k" else 512
+                    project(ps[:, u, :], tiles[(a, b0 + u)][0], tiles[(a, b0 + u)][1], lo, lo + 256)
+                if what == "k":
+                    nc.scalar.copy(
+                        out=k_rows[a][:, :, 8 * b0 : 8 * (b0 + 2)].rearrange("p c (u h) -> p c u h", h=8),
+                        in_=ps[:].rearrange("p u (c h) -> p c u h", h=8),
+                    )
+                else:
+                    nc.scalar.copy(out=v_rows[a][:, b0 : b0 + 2, :, :].rearrange("p b h c -> p b (h c)"), in_=ps[:])
+
+        chunks = [[] for k in range(N_CHUNKS)]
+        col = 0
+        for gi, (hl, wl0, nt) in enumerate(GROUPS):
+            for o in range(25):
+                chunks[col // P].append((gi, o, col % P))
+                col += 8 * nt
+        max_step = {}
+        for k in range(N_CHUNKS):
+            for gi, o, f0 in chunks[k]:
+                max_step[gi] = max(max_step.get(gi, 0), k + 2 if k in VECTOR_REDUCED else k + 4)
+        K_DEAD = {}
+        for k in range(N_CHUNKS):
+            for gi, o, f0 in chunks[k]:
+                K_DEAD[GROUPS[gi][0] + o // 5] = k + K_DEAD_LAG
+        group_of_tile = {}
+        for gi, (hl, wl0, nt) in enumerate(GROUPS):
+            for wl in range(wl0, wl0 + nt):
+                group_of_tile[4 * hl + wl] = gi
+
+        q_banks = {}
+
+        def q_bank(hl, ch):
+            qp = bank([P, 4, 16, 8], F32, "qp", "qp")
+            for wl in range(4):
+                project(
+                    qp[:, wl, :, :].rearrange("p c h -> p (c h)"),
+                    tiles[(hl + 2, wl + 2)][0],
+                    tiles[(hl + 2, wl + 2)][1],
+                    P * ch,
+                    P * (ch + 1),
+                )
+            q_banks[(hl, ch)] = qp
+
+        def rows_of(k):
+            return sorted(set(GROUPS[gi][0] for gi, o, f0 in chunks[k]))
+
+        halves = {}
+
+        def products(k, ch):
+            cs = slice(16 * ch, 16 * (ch + 1))
+            pr = ring_tile([P, 16, P], F32, "pr")
+            todo = list(chunks[k])
+            while todo:
+                gi, o, f0 = todo[0]
+                hl, wl0, nt = GROUPS[gi]
+                i, j = divmod(o, 5)
+                run = 1
+                if nt == 1:
+                    while run < len(todo) and run < 5 - j and todo[run][0] == gi:
+                        run += 1
+                todo = todo[run:]
+                w = 8 * nt * run
+                qv = q_banks[(hl, ch)][:, wl0 : wl0 + nt, :, :].rearrange("p wl c h -> p c wl h")
+                if run > 1:
+                    qv = qv.to_broadcast([P, 16, run, 8])
+                nc.vector.tensor_tensor(
+                    out=pr[:, :, f0 : f0 + w].rearrange("p c (wl h) -> p c wl h", h=8),
+                    in0=qv,
+                    in1=k_rows[hl + i][:, cs, 8 * (wl0 + j) : 8 * (wl0 + j) + w].rearrange("p c (wl h) -> p c wl h", h=8),
+                    op=ALU.mult,
+                )
+            halves[(k, ch)] = pr
+
+        def fold(k):
+            a_ap = halves[(k, 0)][:].rearrange("p c f -> p (c f)")
+            nc.gpsimd.tensor_tensor(out=a_ap, in0=a_ap, in1=halves[(k, 1)][:].rearrange("p c f -> p (c f)"), op=ALU.add)
+            if k in FOLD_TWICE:
+                nc.gpsimd.tensor_tensor(out=a_ap[:, 0:1024], in0=a_ap[:, 0:1024], in1=a_ap[:, 1024:2048], op=ALU.add)
+
+        def left(k):
+            return 8 if k in FOLD_TWICE else 16
+
+        ssbs = {}
+
+        def score_parts(k):
+            parts = []
+            for gi in sorted(set(s[0] for s in chunks[k])):
+                mine = [s for s in chunks[k] if s[0] == gi]
+                w = 8 * GROUPS[gi][2]
+                if gi not in ssbs:
+                    if w < 32:
+                        ssbs[gi] = soft.tile([P, 25, w], F32, name="ssn", tag="ssn", bufs=3)
+                    else:
+                        ssbs[gi] = soft.tile([P, 25, w], F32, name="ssb", tag="ssb")
+                parts.append((ssbs[gi][:, mine[0][1] : mine[-1][1] + 1, :], mine[0][2], mine[-1][2] + w, w))
+            return parts
+
+        def vector_reduce(k):
+            for dst, f0, f1, w in score_parts(k):
+                nc.vector.tensor_reduce(
+                    out=dst,
+                    in_=halves[(k, 0)][:, 0 : left(k), f0:f1].rearrange("p c (s f) -> p s f c", f=w),
+                    axis=AX.X,
+                    op=ALU.add,
+                )
+
+        sts = {}
+
+        def warm(n):
+            for r in range(n):
+                dm = psum.tile([P, 512], F32, name="dm", tag="dm", bufs=1)
+                project(dm[:], wc[:, 0:P], ws[:, 0:P], 256, 768)
+
+        def tensor_reduce(k):
+            st = bank([P, P], F32, "st", "st")
+            for c in range(left(k)):
+                nc.tensor.matmul(
+                    out=st[:],
+                    lhsT=halves[(k, 0)][:, c, :],
+                    rhs=ident_f[:],
+                    is_transpose=True,
+                    start=(c == 0),
+                    stop=(c == left(k) - 1),
+                )
+            sts[k] = st
+
+        def copy_st(k):
+            stsb = soft.tile([P, P], F32, name="stsb", tag="stsb")
+            nc.scalar.copy(out=stsb[:], in_=sts[k][:])
+            sts[k] = stsb
+
+        def back(k):
+            sbp = bank([P, P], F32, "sbp", "st")
+            nc.tensor.transpose(sbp[:], sts[k][:], ident_f[:])
+            sts[k] = sbp
+
+        def copy_back(k):
+            for dst, f0, f1, w in score_parts(k):
+                nc.scalar.copy(out=dst, in_=sts[k][:, f0:f1].rearrange("p (s f) -> p s f", f=w))
+
+        nmxs = {}
+        es = {}
+        sums = {}
+
+        def softmax_max(gi):
+            w = 8 * GROUPS[gi][2]
+            mx = soft.tile([P, w], F32, name="mx", tag="mx")
+            nc.vector.tensor_reduce(out=mx[:], in_=ssbs[gi][:].rearrange("p o f -> p f o"), axis=AX.X, op=ALU.max)
+            nmx = soft.tile([P, w], F32, name="nmx", tag="nmx")
+            nc.vector.tensor_scalar(out=nmx[:], in0=mx[:], scalar1=-1.0, scalar2=None, op0=ALU.mult)
+            nmxs[gi] = nmx
+
+        def softmax_exp(late, gi):
+            w = 8 * GROUPS[gi][2]
+            if w < 32:
+                e = soft.tile([P, w, 25], F32, name="en", tag="en", bufs=3)
+            else:
+                e = late.tile([P, w, 25], F32, name="e", tag="e", bufs=3)
+            ssum = soft.tile([P, w], F32, name="ssum", tag="ssum")
+            for f in range(w):
+                nc.scalar.activation(
+                    out=e[:, f, :],
+                    in_=ssbs[gi][:, :, f],
+                    func=ACT.Exp,
+                    bias=nmxs[gi][:, f : f + 1],
+                    scale=1.0,
+                    accum_out=ssum[:, f : f + 1],
+                )
+            es[gi] = e
+            sums[gi] = ssum
+
+        def softmax_norm(gi):
+            w = 8 * GROUPS[gi][2]
+            rs = soft.tile([P, w], F32, name="rs", tag="rs")
+            nc.vector.reciprocal(out=rs[:], in_=sums[gi][:])
+            nc.vector.tensor_tensor(
+                out=es[gi][:], in0=es[gi][:], in1=rs[:].unsqueeze(2).to_broadcast([P, w, 25]), op=ALU.mult
+            )
+
+        def weights(hl, wl):
+            gi = group_of_tile[4 * hl + wl]
+            f0 = 8 * (wl - GROUPS[gi][1])
+            return es[gi][:, f0 : f0 + 8, :]
+
+        free_tags = ["tmp"] * TMP_BUFS
+        freed_rows = []
+
+        def tmp_tile(late, it):
+            for a in range(8):
+                if it > K_DEAD[a] and a not in freed_rows and len(freed_rows) < K_ROWS_REUSED:
+                    freed_rows.append(a)
+                    free_tags.append("k%d" % a)
+            tag = free_tags.pop(0)
+            if tag == "tmp":
+                tmp = late.tile([P, 5, 8, 32], F32, name="tmp", tag="tmp", bufs=TMP_BUFS)
+            else:
+                tmp = keep.tile([P, 5, 8, 32], F32, name="tmk", tag=tag)
+            return tmp, tag
+
+        def piece_scalar(late, hl, wl, offsets, it):
+            tmp, tag = tmp_tile(late, it)
+            att = weights(hl, wl)
+            for r, o in enumerate(offsets):
+                for h in range(8):
+                    nc.scalar.activation(
+                        out=tmp[:, r, h, :],
+                        in_=v_rows[hl + o // 5][:, wl + o % 5, h, :],
+                        func=ACT.Copy,
+                        scale=att[:, h, o : o + 1],
+                    )
+            return tmp, tag
+
+        def piece_fused(late, hl, wl, offsets):
+            acc = late.tile([P, 1, 8, 32], F32, name="acc", tag="acc", bufs=2)
+            att = weights(hl, wl)
+            for r, o in enumerate(offsets):
+                for h in range(8):
+                    val = v_rows[hl + o // 5][:, wl + o % 5, h, :]
+                    if r == 0:
+                        nc.vector.tensor_scalar(
+                            out=acc[:, 0, h, :], in0=val, scalar1=att[:, h, o : o + 1], scalar2=None, op0=ALU.mult
+                        )
+                    else:
+                        nc.vector.scalar_tensor_tensor(
+                            out=acc[:, 0, h, :],
+                            in0=val,
+                            scalar=att[:, h, o : o + 1],
+                            in1=acc[:, 0, h, :],
+                            op0=ALU.mult,
+                            op1=ALU.add,
+                        )
+            return acc
+
+        def piece_mult(late, hl, wl, i, it):
+            tmp, tag = tmp_tile(late, it)
+            nc.vector.tensor_tensor(
+                out=tmp[:],
+                in0=v_rows[hl + i][:, wl : wl + 5, :, :],
+                in1=weights(hl, wl)[:, :, 5 * i : 5 * (i + 1)]
+                .rearrange("p h j -> p j h")
+                .unsqueeze(3)
+                .to_broadcast([P, 5, 8, 32]),
+                op=ALU.mult,
+            )
+            return tmp, tag
+
+        ots = {}
+        done = {}
+
+        def accumulate(late, g, wl, tmp, n_slices, n_offsets):
+            if g not in ots:
+                ots[g] = [bank([P, 512], F32, "ot%d" % half, "w") for half in range(2)]
+            first = done.get((g, wl), 0) == 0
+            done[(g, wl)] = done.get((g, wl), 0) + n_offsets
+            last = done[(g, wl)] == 25
+            for r in range(n_slices):
+                for half in range(2):
+                    nc.tensor.matmul(
+                        out=ots[g][half][:, P * wl : P * (wl + 1)],
+                        lhsT=tmp[:, r, 4 * half : 4 * (half + 1), :].rearrange("p h c -> p (h c)"),
+                        rhs=ident_f[:],
+                        is_transpose=True,
+                        start=(first and r == 0),
+                        stop=(last and r == n_slices - 1),
+                    )
+            if last and wl == 3:
+                for half in range(2):
+                    ost = late.tile([P, 16, 8, 4], F32, name="ost", tag="ost", bufs=2)
+                    src = ots[g][half][:].rearrange("c (wl m wb) -> c m wb wl", wl=4, wb=8)
+                    if half == 0:
+                        nc.vector.tensor_copy(out=ost[:], in_=src)
+                    else:
+                        nc.scalar.copy(out=ost[:], in_=src)
+                    for n in range(2):
+                        nc.sync.dma_start(
+                            out=out[n, P * half : P * (half + 1)].rearrange("c (hb hl) w -> c hb hl w", hl=4)[:, :, g, :],
+                            in_=ost[:, 8 * n : 8 * (n + 1)].rearrange("c m wb wl -> c m (wb wl)"),
+                        )
+
+        state = {"tile": 0, "offset": 0, "made": [], "exp": [], "norm": [], "ready": -1, "fold": [], "folded": [], "fused": None}
+
+        def step(late, it):
+            k = it - 2
+            on_tensor = 0 <= k < N_CHUNKS and k not in VECTOR_REDUCED
+            back_due = 0 <= k - 1 < N_CHUNKS and k - 1 not in VECTOR_REDUCED
+            folded = []
+            for g, wl, t0, t1 in state["fold"]:
+                a_ap = t0[0][:].rearrange("p j h c -> p (j h c)")
+                nc.gpsimd.tensor_tensor(out=a_ap, in0=a_ap, in1=t1[0][:].rearrange("p j h c -> p (j h c)"), op=ALU.add)
+                free_tags.append(t1[1])
+                folded.append((g, wl, t0, 5, 10))
+            state["fold"] = []
+            if it + 1 < N_CHUNKS:
+                for hl in rows_of(it + 1):
+                    if (hl, 0) not in q_banks:
+                        q_bank(hl, 0)
+            if 0 <= k < N_CHUNKS and k in VECTOR_REDUCED:
+                vector_reduce(k)
+            for gi in range(len(GROUPS)):
+                if max_step[gi] == it:
+                    softmax_max(gi)
+                    state["exp"].append(gi)
+            if it < N_CHUNKS:
+                products(it, 0)
+            for gi in state["norm"]:
+                softmax_norm(gi)
+                state["ready"] = gi
+            state["norm"] = []
+            if it < N_CHUNKS:
+                for hl in rows_of(it):
+                    if (hl, 1) not in q_banks:
+                        q_bank(hl, 1)
+                products(it, 1)
+                fold(it)
+            made = []
+            jobs = []
+            budget = SCALAR_BUDGET - (5 if state["exp"] else 0)
+            while late is not None and budget > 0 and state["tile"] < 16 and group_of_tile[state["tile"]] <= state["ready"]:
+                g, wl = divmod(state["tile"], 4)
+                o = state["offset"]
+                share = VECTOR_OFFSETS if it >= N_CHUNKS else EARLY_OFFSETS
+                if share and (o == 0 or (it >= N_CHUNKS and state["fused"] is None)):
+                    n = ((25 - o) * share + 12) // 25
+                    state["fused"] = (g, wl, None, (piece_fused(late, g, wl, list(range(o, o + n))), None), 1, n)
+                    o += n
+                if it >= N_CHUNKS:
+                    budget = 25 - o
+                n = min(5, 25 - o, budget)
+                while n > 0:
+                    jobs.append((g, wl, list(range(o, o + n)), None, n, n))
+                    budget -= n
+                    o += n
+                    n = min(5, 25 - o, budget)
+                if o == 25:
+                    if state["fused"] is not None:
+                        jobs.append(state["fused"])
+                        state["fused"] = None
+                    state["tile"] += 1
+                    o = 0
+                state["offset"] = o
+                if it >= N_CHUNKS:
+                    budget = 0
+            if it < len(EVACUATIONS):
+                for name in EVACUATIONS[it]:
+                    evacuate(name[0], int(name[1]), ("w",))
+            if on_tensor:
+                tensor_reduce(k)
+                warm(WARMERS)
+            if back_due:
+                back(k - 1)
+            for g, wl, tmp, n_slices, n_offsets in state["folded"] + state["made"]:
+                accumulate(late, g, wl, tmp[0], n_slices, n_offsets)
+                if tmp[1] is not None:
+                    free_tags.append(tmp[1])
+                warm(WARMERS)
+            state["folded"] = folded
+            copies = [on_tensor, back_due]
+
+            def small_copies():
+                if copies[0]:
+                    copy_st(k)
+                if copies[1]:
+                    copy_back(k - 1)
+                copies[0] = False
+                copies[1] = False
+
+            for g, wl, offsets, tmp, n_slices, n_offsets in jobs:
+                if offsets is None:
+                    made.append((g, wl, tmp, n_slices, n_offsets))
+                elif offsets == "mult":
+                    made.append((g, wl, piece_mult(late, g, wl, 0, it), n_slices, n_offsets))
+                else:
+                    made.append((g, wl, piece_scalar(late, g, wl, offsets, it), n_slices, n_offsets))
+                    small_copies()
+            small_copies()
+            for gi in state["exp"]:
+                softmax_exp(late, gi)
+                state["norm"].append(gi)
+            state["exp"] = []
+            if (
+                it < N_CHUNKS
+                and it % FOLD_EVERY == 0
+                and len(made) == 2
+                and made[0][:2] == made[1][:2]
+                and made[0][3] == 5
+                and made[1][3] == 5
+            ):
+                state["fold"].append((made[0][0], made[0][1], made[0][2], made[1][2]))
+                made = []
+            state["made"] = made
+
+        with tc.tile_pool(name="codes", bufs=1) as codes:
+            every = ("w", "qp", "st")
+            g2 = gather_row(2)
+            g4 = gather_row(4)
+            quantise_row(codes, 2, g2)
+            evacuate("k", 2, every)
+            g5 = gather_row(5)
+            quantise_row(codes, 4, g4)
+            move_row(codes, 0)
+            evacuate("k", 0, every)
+            g3 = gather_row(3)
+            quantise_row(codes, 5, g5)
+            move_row(codes, 1)
+            evacuate("k", 1, every)
+            quantise_row(codes, 3, g3)
+            evacuate("k", 3, every)
+            evacuate("k", 4, every)
+            q_bank(0, 0)
+            move_row(codes, 6)
+            move_row(codes, 7)
+            for it in range(len(EVACUATIONS)):
+                step(None, it)
+        with tc.tile_pool(name="late", bufs=4) as late:
+            it = len(EVACUATIONS)
+            while state["tile"] < 16 or state["made"] or state["fold"] or state["folded"]:
+                step(late, it)
+                it += 1

@@ -17,19 +17,26 @@ P = 128
 FLOPS = 2 * 768 * 512 * 2048 + 2 * 2 * 2048 * 8 * 25 * 32
 
 N_CHUNKS = 25
-GROUPS = ((0, 0, 1), (0, 1, 1), (0, 2, 2), (1, 0, 4), (2, 0, 4), (3, 0, 4))
-VECTOR_REDUCED = (1, 3, 6, 12, 18, 23, 24)
-EVACUATIONS = (("v0", "v1"), ("v2", "v3"), ("v4", "k5"), ("k6", "k7"), ("v5", "v6", "v7"))
-WARMERS = 0
-FOLD_TWICE = ()
-VECTOR_OFFSETS = 13
-VECTOR_MULT = 0
-SCALAR_BUDGET = 10
-TMP_BUFS = 3
-FOLD_EVERY = 99
-EARLY_OFFSETS = 0
-K_DEAD_LAG = 0
-K_ROWS_REUSED = 2
+GPSIMD_EVERY = 4
+SCALAR_BUDGET = 4
+SCALAR_SHARE = (2, 1)
+TILE_SCORES = 200
+
+
+def segments(k):
+    out = []
+    u = 16 * k
+    while u < 16 * (k + 1):
+        tile, o = divmod(u, 25)
+        i, j = divmod(o, 5)
+        n = min(5 - j, 16 * (k + 1) - u)
+        out.append((tile, i, j, n, 8 * (u - 16 * k)))
+        u += n
+    return out
+
+
+def last_chunk(tile):
+    return (TILE_SCORES * (tile + 1) - 1) // P
 
 
 def tile_relation_kernel(tc, x, w_qkv, out):
@@ -37,7 +44,7 @@ def tile_relation_kernel(tc, x, w_qkv, out):
     with ExitStack() as ctx:
         ctx.enter_context(tc.manual_schedule())
         keep = ctx.enter_context(tc.tile_pool(name="keep", bufs=1))
-        ring = ctx.enter_context(tc.tile_pool(name="ring", bufs=5))
+        ring = ctx.enter_context(tc.tile_pool(name="ring", bufs=6))
         soft = ctx.enter_context(tc.tile_pool(name="soft", bufs=2))
         psum = ctx.enter_context(tc.psum_pool(name="psum", bufs=2))
 
@@ -50,7 +57,9 @@ def tile_relation_kernel(tc, x, w_qkv, out):
         core_c = [keep.tile([P, 512], U32, name="cc%d" % r, align_bytes=64) for r in range(4)]
         core_s = [keep.tile([P, 512], U8, name="cs%d" % r, align_bytes=64) for r in range(4)]
 
-        bank_bufs = {"w": 3, "qp": 3, "st": 2}
+        e_parts = [keep.tile([P, 8, 8, 25], F32, name="e_lo")]
+        sums = keep.tile([P, 16, 8], F32, name="sums")
+        bank_bufs = {"w": 2, "qp": 4, "st": 2}
 
         def bank(shape, dtype, name, tag):
             return psum.tile(shape, dtype, name=name, tag=tag, bufs=bank_bufs[tag])
@@ -174,8 +183,8 @@ def tile_relation_kernel(tc, x, w_qkv, out):
                         nc.vector.tensor_copy(out=dst[:, rows, 0 : width - sh], in_=src[:, :, sh:width])
             name_tiles(a, ((0, 8, hc[:], hs[:]),))
 
-        def evacuate(what, a, tags):
-            for r, b0 in enumerate((0, 2, 4, 6)):
+        def evacuate(what, a, tags, pairs=(0, 2, 4, 6)):
+            for r, b0 in enumerate(pairs):
                 ps = bank([P, 2, 256], F32, "ps", tags[r % len(tags)])
                 for u in range(2):
                     lo = 256 if what == "k" else 512
@@ -188,28 +197,12 @@ def tile_relation_kernel(tc, x, w_qkv, out):
                 else:
                     nc.scalar.copy(out=v_rows[a][:, b0 : b0 + 2, :, :].rearrange("p b h c -> p b (h c)"), in_=ps[:])
 
-        chunks = [[] for k in range(N_CHUNKS)]
-        col = 0
-        for gi, (hl, wl0, nt) in enumerate(GROUPS):
-            for o in range(25):
-                chunks[col // P].append((gi, o, col % P))
-                col += 8 * nt
-        max_step = {}
-        for k in range(N_CHUNKS):
-            for gi, o, f0 in chunks[k]:
-                max_step[gi] = max(max_step.get(gi, 0), k + 2 if k in VECTOR_REDUCED else k + 4)
-        K_DEAD = {}
-        for k in range(N_CHUNKS):
-            for gi, o, f0 in chunks[k]:
-                K_DEAD[GROUPS[gi][0] + o // 5] = k + K_DEAD_LAG
-        group_of_tile = {}
-        for gi, (hl, wl0, nt) in enumerate(GROUPS):
-            for wl in range(wl0, wl0 + nt):
-                group_of_tile[4 * hl + wl] = gi
-
         q_banks = {}
+        q_copies = {}
 
         def q_bank(hl, ch):
+            if (hl, ch) in q_banks:
+                return
             qp = bank([P, 4, 16, 8], F32, "qp", "qp")
             for wl in range(4):
                 project(
@@ -221,92 +214,51 @@ def tile_relation_kernel(tc, x, w_qkv, out):
                 )
             q_banks[(hl, ch)] = qp
 
+        def q_copy(hl):
+            qs = soft.tile([P, 4, 16, 8], F32, name="qs", tag="qs")
+            nc.scalar.copy(out=qs[:], in_=q_banks[(hl, 0)][:])
+            q_copies[hl] = qs
+
         def rows_of(k):
-            return sorted(set(GROUPS[gi][0] for gi, o, f0 in chunks[k]))
+            return sorted(set(s[0] // 4 for s in segments(k))) if 0 <= k < N_CHUNKS else []
 
         halves = {}
 
-        def products(k, ch):
+        def products(eng, k, ch, q_of):
             cs = slice(16 * ch, 16 * (ch + 1))
             pr = ring_tile([P, 16, P], F32, "pr")
-            todo = list(chunks[k])
-            while todo:
-                gi, o, f0 = todo[0]
-                hl, wl0, nt = GROUPS[gi]
-                i, j = divmod(o, 5)
-                run = 1
-                if nt == 1:
-                    while run < len(todo) and run < 5 - j and todo[run][0] == gi:
-                        run += 1
-                todo = todo[run:]
-                w = 8 * nt * run
-                qv = q_banks[(hl, ch)][:, wl0 : wl0 + nt, :, :].rearrange("p wl c h -> p c wl h")
-                if run > 1:
-                    qv = qv.to_broadcast([P, 16, run, 8])
-                nc.vector.tensor_tensor(
-                    out=pr[:, :, f0 : f0 + w].rearrange("p c (wl h) -> p c wl h", h=8),
+            for tile, i, j, n, f0 in segments(k):
+                hl, wl = divmod(tile, 4)
+                w = 8 * n
+                qv = q_of(hl)[:, wl : wl + 1, :, :].rearrange("p wl c h -> p c wl h")
+                if n > 1:
+                    qv = qv.to_broadcast([P, 16, n, 8])
+                eng.tensor_tensor(
+                    out=pr[:, :, f0 : f0 + w].rearrange("p c (j h) -> p c j h", h=8),
                     in0=qv,
-                    in1=k_rows[hl + i][:, cs, 8 * (wl0 + j) : 8 * (wl0 + j) + w].rearrange("p c (wl h) -> p c wl h", h=8),
+                    in1=k_rows[hl + i][:, cs, 8 * (wl + j) : 8 * (wl + j) + w].rearrange("p c (j h) -> p c j h", h=8),
                     op=ALU.mult,
                 )
             halves[(k, ch)] = pr
 
-        def fold(k):
-            a_ap = halves[(k, 0)][:].rearrange("p c f -> p (c f)")
-            nc.gpsimd.tensor_tensor(out=a_ap, in0=a_ap, in1=halves[(k, 1)][:].rearrange("p c f -> p (c f)"), op=ALU.add)
-            if k in FOLD_TWICE:
-                nc.gpsimd.tensor_tensor(out=a_ap[:, 0:1024], in0=a_ap[:, 0:1024], in1=a_ap[:, 1024:2048], op=ALU.add)
-
-        def left(k):
-            return 8 if k in FOLD_TWICE else 16
-
-        ssbs = {}
-
-        def score_parts(k):
-            parts = []
-            for gi in sorted(set(s[0] for s in chunks[k])):
-                mine = [s for s in chunks[k] if s[0] == gi]
-                w = 8 * GROUPS[gi][2]
-                if gi not in ssbs:
-                    if w < 32:
-                        ssbs[gi] = soft.tile([P, 25, w], F32, name="ssn", tag="ssn", bufs=3)
-                    else:
-                        ssbs[gi] = soft.tile([P, 25, w], F32, name="ssb", tag="ssb")
-                parts.append((ssbs[gi][:, mine[0][1] : mine[-1][1] + 1, :], mine[0][2], mine[-1][2] + w, w))
-            return parts
-
-        def vector_reduce(k):
-            for dst, f0, f1, w in score_parts(k):
-                nc.vector.tensor_reduce(
-                    out=dst,
-                    in_=halves[(k, 0)][:, 0 : left(k), f0:f1].rearrange("p c (s f) -> p s f c", f=w),
-                    axis=AX.X,
-                    op=ALU.add,
-                )
-
         sts = {}
 
-        def warm(n):
-            for r in range(n):
-                dm = psum.tile([P, 512], F32, name="dm", tag="dm", bufs=1)
-                project(dm[:], wc[:, 0:P], ws[:, 0:P], 256, 768)
-
-        def tensor_reduce(k):
-            st = bank([P, P], F32, "st", "st")
-            for c in range(left(k)):
+        def tensor_reduce(k, ch, first, last):
+            if first:
+                sts[k] = bank([P, P], F32, "st", "st")
+            for c in range(16):
                 nc.tensor.matmul(
-                    out=st[:],
-                    lhsT=halves[(k, 0)][:, c, :],
+                    out=sts[k][:],
+                    lhsT=halves[(k, ch)][:, c, :],
                     rhs=ident_f[:],
                     is_transpose=True,
-                    start=(c == 0),
-                    stop=(c == left(k) - 1),
+                    start=(first and c == 0),
+                    stop=(last and c == 15),
                 )
-            sts[k] = st
 
         def copy_st(k):
             stsb = soft.tile([P, P], F32, name="stsb", tag="stsb")
-            nc.scalar.copy(out=stsb[:], in_=sts[k][:])
+            nc.scalar.activation(out=stsb[:], in_=sts[k][:], func=ACT.Copy, scale=-1.0)
             sts[k] = stsb
 
         def back(k):
@@ -314,126 +266,86 @@ def tile_relation_kernel(tc, x, w_qkv, out):
             nc.tensor.transpose(sbp[:], sts[k][:], ident_f[:])
             sts[k] = sbp
 
+        scores = {}
+
         def copy_back(k):
-            for dst, f0, f1, w in score_parts(k):
-                nc.scalar.copy(out=dst, in_=sts[k][:, f0:f1].rearrange("p (s f) -> p s f", f=w))
+            lo = P * k
+            while lo < P * (k + 1):
+                tile = lo // TILE_SCORES
+                hi = min(P * (k + 1), TILE_SCORES * (tile + 1))
+                if tile not in scores:
+                    scores[tile] = soft.tile([P, 25, 8], F32, name="sc", tag="sc", bufs=4)
+                a, b = lo - TILE_SCORES * tile, hi - TILE_SCORES * tile
+                nc.scalar.copy(out=scores[tile][:, a // 8 : b // 8, :].rearrange("p o h -> p (o h)"), in_=sts[k][:, lo - P * k : hi - P * k])
+                lo = hi
 
-        nmxs = {}
-        es = {}
-        sums = {}
+        minima = {}
 
-        def softmax_max(gi):
-            w = 8 * GROUPS[gi][2]
-            mx = soft.tile([P, w], F32, name="mx", tag="mx")
-            nc.vector.tensor_reduce(out=mx[:], in_=ssbs[gi][:].rearrange("p o f -> p f o"), axis=AX.X, op=ALU.max)
-            nmx = soft.tile([P, w], F32, name="nmx", tag="nmx")
-            nc.vector.tensor_scalar(out=nmx[:], in0=mx[:], scalar1=-1.0, scalar2=None, op0=ALU.mult)
-            nmxs[gi] = nmx
+        def weights(tile):
+            return e_parts[tile // 8][:, tile % 8, :, :]
 
-        def softmax_exp(late, gi):
-            w = 8 * GROUPS[gi][2]
-            if w < 32:
-                e = soft.tile([P, w, 25], F32, name="en", tag="en", bufs=3)
-            else:
-                e = late.tile([P, w, 25], F32, name="e", tag="e", bufs=3)
-            ssum = soft.tile([P, w], F32, name="ssum", tag="ssum")
-            for f in range(w):
+        def softmax_max(tile):
+            mn = soft.tile([P, 8], F32, name="mn", tag="mn")
+            nc.vector.tensor_reduce(out=mn[:], in_=scores[tile][:].rearrange("p o h -> p h o"), axis=AX.X, op=ALU.min)
+            minima[tile] = mn
+
+        def softmax_exp(tile):
+            for h in range(8):
                 nc.scalar.activation(
-                    out=e[:, f, :],
-                    in_=ssbs[gi][:, :, f],
+                    out=weights(tile)[:, h, :],
+                    in_=scores[tile][:, :, h],
                     func=ACT.Exp,
-                    bias=nmxs[gi][:, f : f + 1],
-                    scale=1.0,
-                    accum_out=ssum[:, f : f + 1],
+                    bias=minima[tile][:, h : h + 1],
+                    scale=-1.0,
+                    accum_out=sums[:, tile, h : h + 1],
                 )
-            es[gi] = e
-            sums[gi] = ssum
 
-        def softmax_norm(gi):
-            w = 8 * GROUPS[gi][2]
-            rs = soft.tile([P, w], F32, name="rs", tag="rs")
-            nc.vector.reciprocal(out=rs[:], in_=sums[gi][:])
+        def softmax_recip(tile):
+            nc.vector.reciprocal(out=sums[:, tile, :], in_=sums[:, tile, :])
+
+        def softmax_norm(tile):
             nc.vector.tensor_tensor(
-                out=es[gi][:], in0=es[gi][:], in1=rs[:].unsqueeze(2).to_broadcast([P, w, 25]), op=ALU.mult
+                out=weights(tile),
+                in0=weights(tile),
+                in1=sums[:, tile, :].unsqueeze(2).to_broadcast([P, 8, 25]),
+                op=ALU.mult,
             )
 
-        def weights(hl, wl):
-            gi = group_of_tile[4 * hl + wl]
-            f0 = 8 * (wl - GROUPS[gi][1])
-            return es[gi][:, f0 : f0 + 8, :]
-
-        free_tags = ["tmp"] * TMP_BUFS
-        freed_rows = []
-
-        def tmp_tile(late, it):
-            for a in range(8):
-                if it > K_DEAD[a] and a not in freed_rows and len(freed_rows) < K_ROWS_REUSED:
-                    freed_rows.append(a)
-                    free_tags.append("k%d" % a)
-            tag = free_tags.pop(0)
-            if tag == "tmp":
-                tmp = late.tile([P, 5, 8, 32], F32, name="tmp", tag="tmp", bufs=TMP_BUFS)
-            else:
-                tmp = keep.tile([P, 5, 8, 32], F32, name="tmk", tag=tag)
-            return tmp, tag
-
-        def piece_scalar(late, hl, wl, offsets, it):
-            tmp, tag = tmp_tile(late, it)
-            att = weights(hl, wl)
+        def piece_scalar(late, tile, offsets):
+            hl, wl = divmod(tile, 4)
+            tmp = late.tile([P, 5, 8, 32], F32, name="tmp", tag="tmp", bufs=4)
             for r, o in enumerate(offsets):
                 for h in range(8):
                     nc.scalar.activation(
                         out=tmp[:, r, h, :],
                         in_=v_rows[hl + o // 5][:, wl + o % 5, h, :],
                         func=ACT.Copy,
-                        scale=att[:, h, o : o + 1],
+                        scale=weights(tile)[:, h, o : o + 1],
                     )
-            return tmp, tag
+            return tmp
 
-        def piece_fused(late, hl, wl, offsets):
-            acc = late.tile([P, 1, 8, 32], F32, name="acc", tag="acc", bufs=2)
-            att = weights(hl, wl)
-            for r, o in enumerate(offsets):
-                for h in range(8):
-                    val = v_rows[hl + o // 5][:, wl + o % 5, h, :]
-                    if r == 0:
-                        nc.vector.tensor_scalar(
-                            out=acc[:, 0, h, :], in0=val, scalar1=att[:, h, o : o + 1], scalar2=None, op0=ALU.mult
-                        )
-                    else:
-                        nc.vector.scalar_tensor_tensor(
-                            out=acc[:, 0, h, :],
-                            in0=val,
-                            scalar=att[:, h, o : o + 1],
-                            in1=acc[:, 0, h, :],
-                            op0=ALU.mult,
-                            op1=ALU.add,
-                        )
-            return acc
-
-        def piece_mult(late, hl, wl, i, it):
-            tmp, tag = tmp_tile(late, it)
+        def piece_vector(tile, i):
+            hl, wl = divmod(tile, 4)
+            tmp = ring_tile([P, 5, 8, 32], F32, "tmv")
             nc.vector.tensor_tensor(
                 out=tmp[:],
                 in0=v_rows[hl + i][:, wl : wl + 5, :, :],
-                in1=weights(hl, wl)[:, :, 5 * i : 5 * (i + 1)]
-                .rearrange("p h j -> p j h")
-                .unsqueeze(3)
-                .to_broadcast([P, 5, 8, 32]),
+                in1=weights(tile)[:, :, 5 * i : 5 * (i + 1)].rearrange("p h j -> p j h").unsqueeze(3).to_broadcast([P, 5, 8, 32]),
                 op=ALU.mult,
             )
-            return tmp, tag
+            return tmp
 
         ots = {}
         done = {}
 
-        def accumulate(late, g, wl, tmp, n_slices, n_offsets):
+        def accumulate(late, tile, tmp, n, tag):
+            g, wl = divmod(tile, 4)
             if g not in ots:
-                ots[g] = [bank([P, 512], F32, "ot%d" % half, "w") for half in range(2)]
-            first = done.get((g, wl), 0) == 0
-            done[(g, wl)] = done.get((g, wl), 0) + n_offsets
-            last = done[(g, wl)] == 25
-            for r in range(n_slices):
+                ots[g] = [bank([P, 512], F32, "ot%d" % half, tag) for half in range(2)]
+            first = done.get(tile, 0) == 0
+            done[tile] = done.get(tile, 0) + n
+            last = done[tile] == 25
+            for r in range(n):
                 for half in range(2):
                     nc.tensor.matmul(
                         out=ots[g][half][:, P * wl : P * (wl + 1)],
@@ -441,7 +353,7 @@ def tile_relation_kernel(tc, x, w_qkv, out):
                         rhs=ident_f[:],
                         is_transpose=True,
                         start=(first and r == 0),
-                        stop=(last and r == n_slices - 1),
+                        stop=(last and r == n - 1),
                     )
             if last and wl == 3:
                 for half in range(2):
@@ -451,123 +363,72 @@ def tile_relation_kernel(tc, x, w_qkv, out):
                         nc.vector.tensor_copy(out=ost[:], in_=src)
                     else:
                         nc.scalar.copy(out=ost[:], in_=src)
-                    for n in range(2):
+                    for n_img in range(2):
                         nc.sync.dma_start(
-                            out=out[n, P * half : P * (half + 1)].rearrange("c (hb hl) w -> c hb hl w", hl=4)[:, :, g, :],
-                            in_=ost[:, 8 * n : 8 * (n + 1)].rearrange("c m wb wl -> c m (wb wl)"),
+                            out=out[n_img, P * half : P * (half + 1)].rearrange("c (hb hl) w -> c hb hl w", hl=4)[:, :, g, :],
+                            in_=ost[:, 8 * n_img : 8 * (n_img + 1)].rearrange("c m wb wl -> c m (wb wl)"),
                         )
 
-        state = {"tile": 0, "offset": 0, "made": [], "exp": [], "norm": [], "ready": -1, "fold": [], "folded": [], "fused": None}
+        due = {}
+        for tile in range(16):
+            due.setdefault(last_chunk(tile) + 3, []).append(tile)
+        evacuations = [("v", a, b) for a in range(5) for b in (0, 2, 4, 6)]
+        for name, a in (("k", 5), ("k", 6), ("v", 5), ("k", 7), ("v", 6), ("v", 7)):
+            evacuations += [(name, a, b) for b in (0, 2, 4, 6)]
+        state = {"tile": 0, "offset": 0, "ready": -1, "made": []}
 
         def step(late, it):
-            k = it - 2
-            on_tensor = 0 <= k < N_CHUNKS and k not in VECTOR_REDUCED
-            back_due = 0 <= k - 1 < N_CHUNKS and k - 1 not in VECTOR_REDUCED
-            folded = []
-            for g, wl, t0, t1 in state["fold"]:
-                a_ap = t0[0][:].rearrange("p j h c -> p (j h c)")
-                nc.gpsimd.tensor_tensor(out=a_ap, in0=a_ap, in1=t1[0][:].rearrange("p j h c -> p (j h c)"), op=ALU.add)
-                free_tags.append(t1[1])
-                folded.append((g, wl, t0, 5, 10))
-            state["fold"] = []
-            if it + 1 < N_CHUNKS:
-                for hl in rows_of(it + 1):
-                    if (hl, 0) not in q_banks:
-                        q_bank(hl, 0)
-            if 0 <= k < N_CHUNKS and k in VECTOR_REDUCED:
-                vector_reduce(k)
-            for gi in range(len(GROUPS)):
-                if max_step[gi] == it:
-                    softmax_max(gi)
-                    state["exp"].append(gi)
-            if it < N_CHUNKS:
-                products(it, 0)
-            for gi in state["norm"]:
-                softmax_norm(gi)
-                state["ready"] = gi
-            state["norm"] = []
-            if it < N_CHUNKS:
-                for hl in rows_of(it):
-                    if (hl, 1) not in q_banks:
-                        q_bank(hl, 1)
-                products(it, 1)
-                fold(it)
-            made = []
-            jobs = []
-            budget = SCALAR_BUDGET - (5 if state["exp"] else 0)
-            while late is not None and budget > 0 and state["tile"] < 16 and group_of_tile[state["tile"]] <= state["ready"]:
-                g, wl = divmod(state["tile"], 4)
-                o = state["offset"]
-                share = VECTOR_OFFSETS if it >= N_CHUNKS else EARLY_OFFSETS
-                if share and (o == 0 or (it >= N_CHUNKS and state["fused"] is None)):
-                    n = ((25 - o) * share + 12) // 25
-                    state["fused"] = (g, wl, None, (piece_fused(late, g, wl, list(range(o, o + n))), None), 1, n)
-                    o += n
-                if it >= N_CHUNKS:
-                    budget = 25 - o
-                n = min(5, 25 - o, budget)
-                while n > 0:
-                    jobs.append((g, wl, list(range(o, o + n)), None, n, n))
-                    budget -= n
-                    o += n
-                    n = min(5, 25 - o, budget)
-                if o == 25:
-                    if state["fused"] is not None:
-                        jobs.append(state["fused"])
-                        state["fused"] = None
-                    state["tile"] += 1
-                    o = 0
-                state["offset"] = o
-                if it >= N_CHUNKS:
-                    budget = 0
-            if it < len(EVACUATIONS):
-                for name in EVACUATIONS[it]:
-                    evacuate(name[0], int(name[1]), ("w",))
-            if on_tensor:
-                tensor_reduce(k)
-                warm(WARMERS)
-            if back_due:
-                back(k - 1)
-            for g, wl, tmp, n_slices, n_offsets in state["folded"] + state["made"]:
-                accumulate(late, g, wl, tmp[0], n_slices, n_offsets)
-                if tmp[1] is not None:
-                    free_tags.append(tmp[1])
-                warm(WARMERS)
-            state["folded"] = folded
-            copies = [on_tensor, back_due]
-
-            def small_copies():
-                if copies[0]:
-                    copy_st(k)
-                if copies[1]:
-                    copy_back(k - 1)
-                copies[0] = False
-                copies[1] = False
-
-            for g, wl, offsets, tmp, n_slices, n_offsets in jobs:
-                if offsets is None:
-                    made.append((g, wl, tmp, n_slices, n_offsets))
-                elif offsets == "mult":
-                    made.append((g, wl, piece_mult(late, g, wl, 0, it), n_slices, n_offsets))
+            on = 0 <= it < N_CHUNKS
+            red = 0 <= it - 1 < N_CHUNKS
+            bk = 0 <= it - 2 < N_CHUNKS
+            for hl in rows_of(it + 1):
+                if (hl, 0) not in q_banks:
+                    q_bank(hl, 0)
+                    q_copy(hl)
+                    q_bank(hl, 1)
+            count = 5
+            for name, a, b0 in evacuations[:count]:
+                evacuate(name, a, ("w",), (b0,))
+            evacuations[:count] = []
+            for tile, tmp, n in state["made"]:
+                accumulate(late, tile, tmp, n, "w")
+            state["made"] = []
+            for tile in due.get(it, []):
+                softmax_max(tile)
+            for tile in due.get(it - 1, []):
+                softmax_recip(tile)
+            if on:
+                if it % GPSIMD_EVERY != GPSIMD_EVERY - 1:
+                    products(nc.gpsimd, it, 0, lambda hl: q_copies[hl])
                 else:
-                    made.append((g, wl, piece_scalar(late, g, wl, offsets, it), n_slices, n_offsets))
-                    small_copies()
-            small_copies()
-            for gi in state["exp"]:
-                softmax_exp(late, gi)
-                state["norm"].append(gi)
-            state["exp"] = []
-            if (
-                it < N_CHUNKS
-                and it % FOLD_EVERY == 0
-                and len(made) == 2
-                and made[0][:2] == made[1][:2]
-                and made[0][3] == 5
-                and made[1][3] == 5
-            ):
-                state["fold"].append((made[0][0], made[0][1], made[0][2], made[1][2]))
-                made = []
-            state["made"] = made
+                    products(nc.vector, it, 0, lambda hl: q_banks[(hl, 0)])
+            for tile in due.get(it - 1, []):
+                softmax_norm(tile)
+            if on:
+                products(nc.vector, it, 1, lambda hl: q_banks[(hl, 1)])
+            if red:
+                tensor_reduce(it - 1, 1, True, False)
+            if bk:
+                back(it - 2)
+            if red:
+                tensor_reduce(it - 1, 0, False, True)
+            budget = SCALAR_BUDGET
+            if late is None or state["tile"] > state["ready"]:
+                budget = 0
+            if bk:
+                copy_back(it - 2)
+            while budget > 0 and state["tile"] <= state["ready"]:
+                o = state["offset"]
+                n = min(5 - o % 5, budget)
+                tmp = piece_scalar(late, state["tile"], list(range(o, o + n)))
+                state["made"].append((state["tile"], tmp, n))
+                budget -= n
+                state["tile"], state["offset"] = divmod(25 * state["tile"] + o + n, 25)
+            if red:
+                copy_st(it - 1)
+            for tile in due.get(it, []):
+                softmax_exp(tile)
+            state["ready"] = max([state["ready"]] + due.get(it - 1, []))
 
         with tc.tile_pool(name="codes", bufs=1) as codes:
             every = ("w", "qp", "st")
@@ -587,12 +448,35 @@ def tile_relation_kernel(tc, x, w_qkv, out):
             evacuate("k", 3, every)
             evacuate("k", 4, every)
             q_bank(0, 0)
+            q_copy(0)
+            q_bank(0, 1)
             move_row(codes, 6)
             move_row(codes, 7)
-            for it in range(len(EVACUATIONS)):
+            it = 0
+            while evacuations:
                 step(None, it)
+                it += 1
         with tc.tile_pool(name="late", bufs=4) as late:
-            it = len(EVACUATIONS)
-            while state["tile"] < 16 or state["made"] or state["fold"] or state["folded"]:
+            e_parts.append(late.tile([P, 8, 8, 25], F32, name="e_hi", tag="e_hi", bufs=1))
+            while it < N_CHUNKS + 4:
                 step(late, it)
                 it += 1
+            tile = state["tile"]
+            while tile < 16:
+                o = state["offset"] if tile == state["tile"] else 0
+                todo = list(range(o, 25))
+                pieces = []
+                if o % 5:
+                    pieces.append(("s", list(range(o, o + 5 - o % 5))))
+                rows = list(range((o + 4) // 5, 5))
+                n_scalar = len(rows) * SCALAR_SHARE[tile % len(SCALAR_SHARE)] // 5
+                for r, i in enumerate(rows):
+                    pieces.append(("s" if r < n_scalar else "v", list(range(5 * i, 5 * i + 5))))
+                made = state["made"]
+                state["made"] = []
+                for kind, offsets in pieces:
+                    tmp = piece_scalar(late, tile, offsets) if kind == "s" else piece_vector(tile, offsets[0] // 5)
+                    made.append((tile, tmp, len(offsets)))
+                for t, tmp, n in sorted(made, key=lambda m: m[0]):
+                    accumulate(late, t, tmp, n, ("w", "qp")[(t // 4) % 2])
+                tile += 1

@@ -324,13 +324,26 @@ def tile_relation_kernel(tc, x, w_qkv, out):
                     )
             return tmp
 
+        psum_weights = {}
+
+        def weights_to_psum(tile):
+            wp = bank([P, 8, 25], F32, "wp", "st")
+            nc.tensor.matmul(
+                out=wp[:].rearrange("p h o -> p (h o)"),
+                lhsT=ident_f[:],
+                rhs=weights(tile).rearrange("p h o -> p (h o)"),
+                start=True,
+                stop=True,
+            )
+            psum_weights[tile] = wp
+
         def piece_vector(tile, i):
             hl, wl = divmod(tile, 4)
             tmp = ring_tile([P, 5, 8, 32], F32, "tmv")
             nc.vector.tensor_tensor(
                 out=tmp[:],
                 in0=v_rows[hl + i][:, wl : wl + 5, :, :],
-                in1=weights(tile)[:, :, 5 * i : 5 * (i + 1)].rearrange("p h j -> p j h").unsqueeze(3).to_broadcast([P, 5, 8, 32]),
+                in1=psum_weights[tile][:, :, 5 * i : 5 * (i + 1)].rearrange("p h j -> p j h").unsqueeze(3).to_broadcast([P, 5, 8, 32]),
                 op=ALU.mult,
             )
             return tmp
@@ -462,6 +475,7 @@ def tile_relation_kernel(tc, x, w_qkv, out):
                 step(late, it)
                 it += 1
             tile = state["tile"]
+            weights_to_psum(tile)
             while tile < 16:
                 o = state["offset"] if tile == state["tile"] else 0
                 todo = list(range(o, 25))
@@ -477,6 +491,8 @@ def tile_relation_kernel(tc, x, w_qkv, out):
                 for kind, offsets in pieces:
                     tmp = piece_scalar(late, tile, offsets) if kind == "s" else piece_vector(tile, offsets[0] // 5)
                     made.append((tile, tmp, len(offsets)))
+                if tile < 15:
+                    weights_to_psum(tile + 1)
                 for t, tmp, n in sorted(made, key=lambda m: m[0]):
                     accumulate(late, t, tmp, n, ("w", "qp")[(t // 4) % 2])
                 tile += 1

@@ -17,8 +17,8 @@ P = 128
 FLOPS = 2 * 768 * 512 * 2048 + 2 * 2 * 2048 * 8 * 25 * 32
 
 N_CHUNKS = 25
-GPSIMD_EVERY = 4
-SCALAR_BUDGET = 4
+EVACUATIONS = 4
+SCALAR_BUDGET = 6
 SCALAR_SHARE = (2, 1)
 TILE_SCORES = 200
 
@@ -33,6 +33,14 @@ def segments(k):
         out.append((tile, i, j, n, 8 * (u - 16 * k)))
         u += n
     return out
+
+
+def gpsimd_multiplies(k):
+    return k % 4 == 0
+
+
+def gpsimd_adds(k):
+    return k % 4 != 0 and k % 8 != 2
 
 
 def last_chunk(tile):
@@ -59,7 +67,7 @@ def tile_relation_kernel(tc, x, w_qkv, out):
 
         e_parts = [keep.tile([P, 8, 8, 25], F32, name="e_lo")]
         sums = keep.tile([P, 16, 8], F32, name="sums")
-        bank_bufs = {"w": 2, "qp": 4, "st": 2}
+        bank_bufs = {"w": 2, "qa": 2, "qb": 2, "st": 2}
 
         def bank(shape, dtype, name, tag):
             return psum.tile(shape, dtype, name=name, tag=tag, bufs=bank_bufs[tag])
@@ -203,7 +211,7 @@ def tile_relation_kernel(tc, x, w_qkv, out):
         def q_bank(hl, ch):
             if (hl, ch) in q_banks:
                 return
-            qp = bank([P, 4, 16, 8], F32, "qp", "qp")
+            qp = bank([P, 4, 16, 8], F32, "qp", ("qa", "qb")[ch])
             for wl in range(4):
                 project(
                     qp[:, wl, :, :].rearrange("p c h -> p (c h)"),
@@ -243,18 +251,23 @@ def tile_relation_kernel(tc, x, w_qkv, out):
 
         sts = {}
 
-        def tensor_reduce(k, ch, first, last):
-            if first:
-                sts[k] = bank([P, P], F32, "st", "st")
-            for c in range(16):
-                nc.tensor.matmul(
-                    out=sts[k][:],
-                    lhsT=halves[(k, ch)][:, c, :],
-                    rhs=ident_f[:],
-                    is_transpose=True,
-                    start=(first and c == 0),
-                    stop=(last and c == 15),
-                )
+        def fold(k):
+            a_ap = halves[(k, 0)][:].rearrange("p c f -> p (c f)")
+            nc.gpsimd.tensor_tensor(out=a_ap, in0=a_ap, in1=halves[(k, 1)][:].rearrange("p c f -> p (c f)"), op=ALU.add)
+
+        def tensor_reduce(k):
+            parts = (0,) if gpsimd_adds(k) else (1, 0)
+            sts[k] = bank([P, P], F32, "st", "st")
+            for ch in parts:
+                for c in range(16):
+                    nc.tensor.matmul(
+                        out=sts[k][:],
+                        lhsT=halves[(k, ch)][:, c, :],
+                        rhs=ident_f[:],
+                        is_transpose=True,
+                        start=(ch == parts[0] and c == 0),
+                        stop=(ch == parts[-1] and c == 15),
+                    )
 
         def copy_st(k):
             stsb = soft.tile([P, P], F32, name="stsb", tag="stsb")
@@ -327,7 +340,7 @@ def tile_relation_kernel(tc, x, w_qkv, out):
         psum_weights = {}
 
         def weights_to_psum(tile):
-            wp = bank([P, 8, 25], F32, "wp", "st")
+            wp = bank([P, 8, 25], F32, "wp", "qa")
             nc.tensor.matmul(
                 out=wp[:].rearrange("p h o -> p (h o)"),
                 lhsT=ident_f[:],
@@ -337,9 +350,13 @@ def tile_relation_kernel(tc, x, w_qkv, out):
             )
             psum_weights[tile] = wp
 
+        spare = ["k%d" % r for r in range(8)]
+
         def piece_vector(tile, i):
             hl, wl = divmod(tile, 4)
-            tmp = ring_tile([P, 5, 8, 32], F32, "tmv")
+            tag = spare.pop(0)
+            spare.append(tag)
+            tmp = keep.tile([P, 5, 8, 32], F32, name="tmv", tag=tag)
             nc.vector.tensor_tensor(
                 out=tmp[:],
                 in0=v_rows[hl + i][:, wl : wl + 5, :, :],
@@ -348,15 +365,19 @@ def tile_relation_kernel(tc, x, w_qkv, out):
             )
             return tmp
 
+        def add_pieces(t0, t1):
+            a_ap = t0[:].rearrange("p j h c -> p (j h c)")
+            nc.gpsimd.tensor_tensor(out=a_ap, in0=a_ap, in1=t1[:].rearrange("p j h c -> p (j h c)"), op=ALU.add)
+
         ots = {}
         done = {}
 
-        def accumulate(late, tile, tmp, n, tag):
+        def accumulate(late, tile, tmp, n, covers):
             g, wl = divmod(tile, 4)
             if g not in ots:
-                ots[g] = [bank([P, 512], F32, "ot%d" % half, tag) for half in range(2)]
+                ots[g] = [bank([P, 512], F32, "ot%d" % half, ("w", "qb")[g % 2]) for half in range(2)]
             first = done.get(tile, 0) == 0
-            done[tile] = done.get(tile, 0) + n
+            done[tile] = done.get(tile, 0) + covers
             last = done[tile] == 25
             for r in range(n):
                 for half in range(2):
@@ -369,7 +390,11 @@ def tile_relation_kernel(tc, x, w_qkv, out):
                         stop=(last and r == n - 1),
                     )
             if last and wl == 3:
-                for half in range(2):
+                state["full"].append(g)
+
+        def store(late, g):
+            for half in range(2):
+                if True:
                     ost = late.tile([P, 16, 8, 4], F32, name="ost", tag="ost", bufs=2)
                     src = ots[g][half][:].rearrange("c (wl m wb) -> c m wb wl", wl=4, wb=8)
                     if half == 0:
@@ -384,67 +409,100 @@ def tile_relation_kernel(tc, x, w_qkv, out):
 
         due = {}
         for tile in range(16):
-            due.setdefault(last_chunk(tile) + 3, []).append(tile)
-        evacuations = [("v", a, b) for a in range(5) for b in (0, 2, 4, 6)]
-        for name, a in (("k", 5), ("k", 6), ("v", 5), ("k", 7), ("v", 6), ("v", 7)):
-            evacuations += [(name, a, b) for b in (0, 2, 4, 6)]
-        state = {"tile": 0, "offset": 0, "ready": -1, "made": []}
+            due.setdefault(last_chunk(tile) + 4, []).append(tile)
+        evacuations = []
+        for name in ("v0", "v1", "v2", "k5", "v3", "v4", "k6", "v5", "k7", "v6", "v7"):
+            evacuations += [(name[0], int(name[1]), b) for b in (0, 2, 4, 6)]
+        state = {"tile": 0, "offset": 0, "ready": -1, "made": [], "full": [], "wp": None}
 
         def step(late, it):
-            on = 0 <= it < N_CHUNKS
-            red = 0 <= it - 1 < N_CHUNKS
-            bk = 0 <= it - 2 < N_CHUNKS
+            on = it < N_CHUNKS
+            red = 0 <= it - 2 < N_CHUNKS
+            bk = 0 <= it - 3 < N_CHUNKS
             for hl in rows_of(it + 1):
                 if (hl, 0) not in q_banks:
                     q_bank(hl, 0)
                     q_copy(hl)
                     q_bank(hl, 1)
-            count = 5
-            for name, a, b0 in evacuations[:count]:
+            for name, a, b0 in evacuations[:EVACUATIONS]:
                 evacuate(name, a, ("w",), (b0,))
-            evacuations[:count] = []
-            for tile, tmp, n in state["made"]:
-                accumulate(late, tile, tmp, n, "w")
+            evacuations[:EVACUATIONS] = []
+            tile = state["tile"]
+            by_tile = not on and tile < 16
+            full, state["full"] = state["full"], []
+            if by_tile:
+                if state["wp"] is None:
+                    state["wp"] = tile
+                while state["wp"] <= min(15, tile + 1, state["ready"]):
+                    weights_to_psum(state["wp"])
+                    state["wp"] += 1
+            for m in state["made"]:
+                accumulate(late, *m)
             state["made"] = []
-            for tile in due.get(it, []):
-                softmax_max(tile)
-            for tile in due.get(it - 1, []):
-                softmax_recip(tile)
+            for t in due.get(it, []):
+                softmax_max(t)
             if on:
-                if it % GPSIMD_EVERY != GPSIMD_EVERY - 1:
+                for t in due.get(it - 1, []):
+                    softmax_recip(t)
+            if on:
+                if gpsimd_multiplies(it):
                     products(nc.gpsimd, it, 0, lambda hl: q_copies[hl])
                 else:
                     products(nc.vector, it, 0, lambda hl: q_banks[(hl, 0)])
-            for tile in due.get(it - 1, []):
-                softmax_norm(tile)
             if on:
+                for t in due.get(it - 1, []):
+                    softmax_norm(t)
                 products(nc.vector, it, 1, lambda hl: q_banks[(hl, 1)])
-            if red:
-                tensor_reduce(it - 1, 1, True, False)
+                if gpsimd_adds(it):
+                    fold(it)
             if bk:
-                back(it - 2)
+                back(it - 3)
             if red:
-                tensor_reduce(it - 1, 0, False, True)
-            budget = SCALAR_BUDGET
-            if late is None or state["tile"] > state["ready"]:
-                budget = 0
+                tensor_reduce(it - 2)
             if bk:
-                copy_back(it - 2)
-            while budget > 0 and state["tile"] <= state["ready"]:
+                copy_back(it - 3)
+            if not on:
+                for t in due.get(it, []):
+                    softmax_exp(t)
+            if by_tile:
                 o = state["offset"]
-                n = min(5 - o % 5, budget)
-                tmp = piece_scalar(late, state["tile"], list(range(o, o + n)))
-                state["made"].append((state["tile"], tmp, n))
-                budget -= n
-                state["tile"], state["offset"] = divmod(25 * state["tile"] + o + n, 25)
+                rows = list(range((o + 4) // 5, 5))
+                n_scalar = len(rows) * SCALAR_SHARE[tile % len(SCALAR_SHARE)] // 5
+                vs = [piece_vector(tile, i) for i in rows[n_scalar:]]
+                for t in due.get(it - 1, []):
+                    softmax_recip(t)
+                    softmax_norm(t)
+                if o % 5:
+                    n = 5 - o % 5
+                    state["made"].append((tile, piece_scalar(late, tile, list(range(o, o + n))), n, n))
+                for i in rows[:n_scalar]:
+                    state["made"].append((tile, piece_scalar(late, tile, list(range(5 * i, 5 * i + 5))), 5, 5))
+                while len(vs) > 1:
+                    add_pieces(vs[0], vs[1])
+                    state["made"].append((tile, vs[0], 5, 10))
+                    vs = vs[2:]
+                for v in vs:
+                    state["made"].append((tile, v, 5, 5))
+                state["tile"], state["offset"] = tile + 1, 0
+            elif on and late is not None:
+                budget = SCALAR_BUDGET
+                while budget > 0 and state["tile"] <= state["ready"]:
+                    o = state["offset"]
+                    n = min(5 - o % 5, budget)
+                    state["made"].append((state["tile"], piece_scalar(late, state["tile"], list(range(o, o + n))), n, n))
+                    budget -= n
+                    state["tile"], state["offset"] = divmod(25 * state["tile"] + o + n, 25)
             if red:
-                copy_st(it - 1)
-            for tile in due.get(it, []):
-                softmax_exp(tile)
+                copy_st(it - 2)
+            if on:
+                for t in due.get(it, []):
+                    softmax_exp(t)
             state["ready"] = max([state["ready"]] + due.get(it - 1, []))
+            for g in full:
+                store(late, g)
 
         with tc.tile_pool(name="codes", bufs=1) as codes:
-            every = ("w", "qp", "st")
+            every = ("w", "qa", "qb", "st")
             g2 = gather_row(2)
             g4 = gather_row(4)
             quantise_row(codes, 2, g2)
@@ -471,28 +529,6 @@ def tile_relation_kernel(tc, x, w_qkv, out):
                 it += 1
         with tc.tile_pool(name="late", bufs=4) as late:
             e_parts.append(late.tile([P, 8, 8, 25], F32, name="e_hi", tag="e_hi", bufs=1))
-            while it < N_CHUNKS + 4:
+            while it < N_CHUNKS or state["tile"] < 16 or state["made"] or state["full"]:
                 step(late, it)
                 it += 1
-            tile = state["tile"]
-            weights_to_psum(tile)
-            while tile < 16:
-                o = state["offset"] if tile == state["tile"] else 0
-                todo = list(range(o, 25))
-                pieces = []
-                if o % 5:
-                    pieces.append(("s", list(range(o, o + 5 - o % 5))))
-                rows = list(range((o + 4) // 5, 5))
-                n_scalar = len(rows) * SCALAR_SHARE[tile % len(SCALAR_SHARE)] // 5
-                for r, i in enumerate(rows):
-                    pieces.append(("s" if r < n_scalar else "v", list(range(5 * i, 5 * i + 5))))
-                made = state["made"]
-                state["made"] = []
-                for kind, offsets in pieces:
-                    tmp = piece_scalar(late, tile, offsets) if kind == "s" else piece_vector(tile, offsets[0] // 5)
-                    made.append((tile, tmp, len(offsets)))
-                if tile < 15:
-                    weights_to_psum(tile + 1)
-                for t, tmp, n in sorted(made, key=lambda m: m[0]):
-                    accumulate(late, t, tmp, n, ("w", "qp")[(t // 4) % 2])
-                tile += 1

@@ -17,10 +17,16 @@ P = 128
 FLOPS = 2 * 768 * 512 * 2048 + 2 * 2 * 2048 * 8 * 25 * 32
 
 N_CHUNKS = 25
-EVACUATIONS = 4
+TILE_SCORES = 200
+ROW_ORDER = (1, 2, 3, 0)
+GPSIMD_CHANNELS = 12
+EVACUATIONS = 5
 SCALAR_BUDGET = 6
 SCALAR_SHARE = (2, 1)
-TILE_SCORES = 200
+
+
+def window_row(tile, i):
+    return ROW_ORDER[tile // 4] + ((i + 1) % 5 if tile < 4 else i)
 
 
 def segments(k):
@@ -30,17 +36,17 @@ def segments(k):
         tile, o = divmod(u, 25)
         i, j = divmod(o, 5)
         n = min(5 - j, 16 * (k + 1) - u)
-        out.append((tile, i, j, n, 8 * (u - 16 * k)))
+        out.append((tile, window_row(tile, i), j, n, 8 * (u - 16 * k)))
         u += n
     return out
 
 
+def pairs_of(k):
+    return sorted(set(s[0] // 2 for s in segments(k))) if 0 <= k < N_CHUNKS else []
+
+
 def gpsimd_multiplies(k):
     return k % 4 == 0
-
-
-def gpsimd_adds(k):
-    return k % 4 != 0 and k % 8 != 2
 
 
 def last_chunk(tile):
@@ -52,7 +58,7 @@ def tile_relation_kernel(tc, x, w_qkv, out):
     with ExitStack() as ctx:
         ctx.enter_context(tc.manual_schedule())
         keep = ctx.enter_context(tc.tile_pool(name="keep", bufs=1))
-        ring = ctx.enter_context(tc.tile_pool(name="ring", bufs=6))
+        ring = ctx.enter_context(tc.tile_pool(name="ring", bufs=3))
         soft = ctx.enter_context(tc.tile_pool(name="soft", bufs=2))
         psum = ctx.enter_context(tc.psum_pool(name="psum", bufs=2))
 
@@ -62,18 +68,16 @@ def tile_relation_kernel(tc, x, w_qkv, out):
         ws = keep.tile([P, 768], U8, name="ws", align_bytes=64)
         k_rows = [keep.tile([P, 32, 64], F32, name="k%d" % r) for r in range(8)]
         v_rows = [keep.tile([P, 8, 8, 32], F32, name="v%d" % r) for r in range(8)]
-        core_c = [keep.tile([P, 512], U32, name="cc%d" % r, align_bytes=64) for r in range(4)]
-        core_s = [keep.tile([P, 512], U8, name="cs%d" % r, align_bytes=64) for r in range(4)]
-
+        core_c = keep.tile([P, 4, 512], U32, name="core_c", align_bytes=64)
+        core_s = keep.tile([P, 4, 512], U8, name="core_s", align_bytes=64)
         e_parts = [keep.tile([P, 8, 8, 25], F32, name="e_lo")]
         sums = keep.tile([P, 16, 8], F32, name="sums")
-        bank_bufs = {"w": 2, "qa": 2, "qb": 2, "st": 2}
 
         def bank(shape, dtype, name, tag):
-            return psum.tile(shape, dtype, name=name, tag=tag, bufs=bank_bufs[tag])
+            return psum.tile(shape, dtype, name=name, tag=tag, bufs=2)
 
         def ring_tile(shape, dtype, name):
-            return ring.tile(shape, dtype, name=name, tag="b8", align_bytes=64)
+            return ring.tile(shape, dtype, name=name, tag="b16", align_bytes=64)
 
         def project(dst, codes, scales, lo, hi):
             nc.tensor.matmul_mx(
@@ -86,112 +90,53 @@ def tile_relation_kernel(tc, x, w_qkv, out):
                 stop=True,
             )
 
-        wraw = ring_tile([P, 6, 512], BF16, "wraw")
-        nc.sync.dma_start(out=wraw[:], in_=w_qkv.rearrange("(r p) k -> p r k", p=P))
-        raws = []
+        first = ring_tile([P, 8192], BF16, "first")
+        second = ring_tile([P, 8192], BF16, "second")
+        third = ring_tile([P, 8192], BF16, "third")
+        wraw = first[:, 0:3072].rearrange("p (r k) -> p r k", r=6)
+        nc.sync.dma_start(out=wraw, in_=w_qkv.rearrange("(r p) k -> p r k", p=P))
+        raws = [t[:, 4096:8192].rearrange("p (t m) -> p t m", t=4) for t in (first, second)]
         for n in range(2):
-            raw = ring_tile([P, 4, 1024], BF16, "raw%d" % n)
-            nc.sync.dma_start(out=raw[:], in_=x[n].rearrange("(p t) h w -> p t (h w)", t=4))
-            raws.append(raw)
+            nc.sync.dma_start(out=raws[n], in_=x[n].rearrange("(p t) h w -> p t (h w)", t=4))
+        wgrp = second[:, 0:3072]
+        grps = [third[:, 2048 * r : 2048 * (r + 1)] for r in range(4)]
 
-        wgrp = ring_tile([P, 768, 4], BF16, "wgrp")
-        wgrp_f = wgrp[:].rearrange("p w t -> p (w t)").bitcast(F32).rearrange("p (w u) -> p w u", u=2)
-        for r in range(6):
-            ty, hh = divmod(r, 2)
-            words = wraw[:, r, :].bitcast(F32)
-            wt = bank([P, 2, P], F32, "wt", "w")
-            for u in range(2):
-                nc.tensor.transpose(wt[:, u, :], words[:, u:256:2], ident_f[:])
-            if ty < 2:
-                dst = wgrp_f[:, 256 * ty : 256 * (ty + 1), :].rearrange("p (c h) u -> p c h u", h=8)
-                dst = dst[:, :, 4 * hh : 4 * (hh + 1), :]
-                src = wt[:].rearrange("p u (h c) -> p c h u", c=32)
-            else:
-                dst = wgrp_f[:, 512 + P * hh : 512 + P * (hh + 1), :]
-                src = wt[:].rearrange("p u r -> p r u")
-            if r % 2 == 0:
-                nc.vector.tensor_copy(out=dst, in_=src)
-            else:
-                nc.scalar.copy(out=dst, in_=src)
+        def gather(r):
+            dst = grps[r].rearrange("p (c n h w t) -> p c n h w t", c=4, n=2, h=8, w=8)
+            for n, eng, c0, c1 in ((0, nc.vector.tensor_copy, 0, 4), (1, nc.scalar.copy, 2, 4), (1, nc.vector.tensor_copy, 0, 2)):
+                src = raws[n].rearrange("p t (h r w c) -> p r c h w t", h=8, r=4, w=8)
+                eng(out=dst[:, c0:c1, n], in_=src[:, r, c0:c1])
 
-        inters = []
-        for n in range(2):
-            inter = ring_tile([P, 1024, 4], BF16, "inter%d" % n)
-            for eng, lo, hi in ((nc.vector.tensor_copy, 0, 640), (nc.scalar.copy, 640, 1024)):
-                eng(
-                    out=inter[:, lo:hi, :].rearrange("p (c i) t -> p c t i", i=4),
-                    in_=raws[n][:, :, lo:hi].rearrange("p t (c i) -> p c t i", i=4),
-                )
-            inters.append(
-                inter[:]
-                .rearrange("p x t -> p (x t)")
-                .bitcast(F32)
-                .rearrange("p (hb hl wb wl u) -> p hb hl wb wl u", hb=8, hl=4, wb=8, wl=4)
-            )
-            if n == 0:
-                for ty in range(3):
-                    cols = slice(256 * ty, 256 * (ty + 1))
-                    nc.vector.quantize_mx(
-                        out=wc[:, cols].bitcast(FP8X4),
-                        scales=ws[:, cols],
-                        in_=wgrp[:, cols, :].rearrange("p w t -> p (w t)"),
-                    )
+        def quantise(r):
+            nc.vector.quantize_mx(out=core_c[:, r, :].bitcast(FP8X4), scales=core_s[:, r, :], in_=grps[r])
 
-        tiles = {}
-        row_parts = {}
+        def quantise_w(ty):
+            cols = slice(256 * ty, 256 * (ty + 1))
+            nc.vector.quantize_mx(out=wc[:, cols].bitcast(FP8X4), scales=ws[:, cols], in_=wgrp[:, 1024 * ty : 1024 * (ty + 1)])
 
-        def gather_row(a):
-            grp = ring_tile([P, 4096], BF16, "grp")
-            g_f = grp[:].bitcast(F32).rearrange("p (b n hb wb u) -> p b n hb wb u", b=8, n=2, hb=8, wb=8)
-            nc.vector.memset(g_f[:, 0:2, :, :, 0, :], 0.0)
-            nc.vector.memset(g_f[:, 6:8, :, :, 7, :], 0.0)
-            for n in range(2):
-                for bs, wls, wd, wsrc in (
-                    (slice(0, 2), slice(2, 4), slice(1, 8), slice(0, 7)),
-                    (slice(2, 6), slice(0, 4), slice(0, 8), slice(0, 8)),
-                    (slice(6, 8), slice(0, 2), slice(0, 7), slice(1, 8)),
-                ):
-                    nc.vector.tensor_copy(
-                        out=g_f[:, bs, n, :, wd, :],
-                        in_=inters[n][:, :, a - 2, wsrc, wls, :].rearrange("p hb wb wl u -> p wl hb wb u"),
-                    )
-            return grp
+        def move_columns(r0):
+            for dst_t, src_t in ((side_c, core_c), (side_s, core_s)):
+                dst, src = dst_t[:, r0 : r0 + 2, :], src_t[:, r0 : r0 + 2, :]
+                if dst_t is side_c:
+                    dst, src = dst.bitcast(I32), src.bitcast(I32)
+                dst = dst.rearrange("p r (m w) -> p r m w", w=8)
+                src = src.rearrange("p r (m w) -> p r m w", w=8)
+                nc.vector.tensor_copy(out=dst[:, :, 0:32, 1:8], in_=src[:, :, 32:64, 0:7])
+                nc.vector.tensor_copy(out=dst[:, :, 32:64, 0:7], in_=src[:, :, 0:32, 1:8])
 
-        def name_tiles(a, parts):
-            row_parts[a] = parts
-            for b0, b1, c_ap, s_ap in parts:
-                for b in range(b0, b1):
-                    cols = slice(P * (b - b0), P * (b - b0 + 1))
-                    tiles[(a, b)] = (c_ap[:, cols], s_ap[:, cols])
-
-        def quantise_row(codes, a, grp):
-            hc = codes.tile([P, 512], U32, name="hc%d" % a, align_bytes=64)
-            hs = codes.tile([P, 512], U8, name="hs%d" % a, align_bytes=64)
-            parts = (
-                (0, 2, hc[:, 0:256], hs[:, 0:256]),
-                (2, 6, core_c[a - 2][:], core_s[a - 2][:]),
-                (6, 8, hc[:, 256:512], hs[:, 256:512]),
-            )
-            for b0, b1, c_ap, s_ap in parts:
-                nc.vector.quantize_mx(out=c_ap.bitcast(FP8X4), scales=s_ap, in_=grp[:, 512 * b0 : 512 * b1])
-            name_tiles(a, parts)
-
-        def move_row(codes, a):
-            hc = codes.tile([P, 1024], U32, name="hc%d" % a, align_bytes=64)
-            hs = codes.tile([P, 1024], U8, name="hs%d" % a, align_bytes=64)
-            for which, dst_t, width, sh in ((2, hc, 64, 8), (3, hs, 16, 2)):
-                dst = dst_t[:].bitcast(I32).rearrange("p (m x) -> p m x", x=width)
-                nc.vector.memset(dst[:, :, 0:sh] if a < 2 else dst[:, :, width - sh : width], 0)
-                for part in row_parts[a + 4 if a < 2 else a - 4]:
-                    src = part[which].bitcast(I32).rearrange("p (m x) -> p m x", x=width)
-                    rows = slice(2 * part[0], 2 * part[1])
-                    if a < 2:
-                        nc.vector.tensor_copy(out=dst[:, rows, sh:width], in_=src[:, :, 0 : width - sh])
+        def move_rows(up):
+            d0, r0 = (0, 2) if up else (2, 0)
+            for dst_t, core_t, side_t, width, sh in ((edge_c, core_c, side_c, 64, 8), (edge_s, core_s, side_s, 16, 2)):
+                for half, src_t in enumerate((core_t, side_t)):
+                    dst = dst_t[:, d0 : d0 + 2, 512 * half : 512 * (half + 1)].bitcast(I32)
+                    dst = dst.rearrange("p r (m x) -> p r m x", x=width)
+                    src = src_t[:, r0 : r0 + 2, :].bitcast(I32).rearrange("p r (m x) -> p r m x", x=width)
+                    if up:
+                        nc.vector.tensor_copy(out=dst[:, :, :, sh:width], in_=src[:, :, :, 0 : width - sh])
                     else:
-                        nc.vector.tensor_copy(out=dst[:, rows, 0 : width - sh], in_=src[:, :, sh:width])
-            name_tiles(a, ((0, 8, hc[:], hs[:]),))
+                        nc.vector.tensor_copy(out=dst[:, :, :, 0 : width - sh], in_=src[:, :, :, sh:width])
 
-        def evacuate(what, a, tags, pairs=(0, 2, 4, 6)):
+        def evacuate(what, a, tags, pairs=(2, 4, 0, 6)):
             for r, b0 in enumerate(pairs):
                 ps = bank([P, 2, 256], F32, "ps", tags[r % len(tags)])
                 for u in range(2):
@@ -208,66 +153,58 @@ def tile_relation_kernel(tc, x, w_qkv, out):
         q_banks = {}
         q_copies = {}
 
-        def q_bank(hl, ch):
-            if (hl, ch) in q_banks:
-                return
-            qp = bank([P, 4, 16, 8], F32, "qp", ("qa", "qb")[ch])
-            for wl in range(4):
-                project(
-                    qp[:, wl, :, :].rearrange("p c h -> p (c h)"),
-                    tiles[(hl + 2, wl + 2)][0],
-                    tiles[(hl + 2, wl + 2)][1],
-                    P * ch,
-                    P * (ch + 1),
-                )
-            q_banks[(hl, ch)] = qp
+        def q_bank(pair):
+            g, w0 = divmod(2 * pair, 4)
+            qp = bank([P, 2, 32, 8], F32, "qp", "qa")
+            for u in range(2):
+                codes_q, scales_q = tiles[(ROW_ORDER[g] + 2, w0 + u + 2)]
+                project(qp[:, u, :, :].rearrange("p c h -> p (c h)"), codes_q, scales_q, 0, 256)
+            qs = soft.tile([P, 2, GPSIMD_CHANNELS, 8], F32, name="qs", tag="qs")
+            nc.scalar.copy(out=qs[:], in_=qp[:, :, 0:GPSIMD_CHANNELS, :])
+            q_banks[pair] = qp
+            q_copies[pair] = qs
 
-        def q_copy(hl):
-            qs = soft.tile([P, 4, 16, 8], F32, name="qs", tag="qs")
-            nc.scalar.copy(out=qs[:], in_=q_banks[(hl, 0)][:])
-            q_copies[hl] = qs
+        prods = {}
 
-        def rows_of(k):
-            return sorted(set(s[0] // 4 for s in segments(k))) if 0 <= k < N_CHUNKS else []
-
-        halves = {}
-
-        def products(eng, k, ch, q_of):
-            cs = slice(16 * ch, 16 * (ch + 1))
-            pr = ring_tile([P, 16, P], F32, "pr")
-            for tile, i, j, n, f0 in segments(k):
-                hl, wl = divmod(tile, 4)
+        def products(eng, k, c0, c1, q_of):
+            for tile, a, j, n, f0 in segments(k):
+                u = tile % 2
                 w = 8 * n
-                qv = q_of(hl)[:, wl : wl + 1, :, :].rearrange("p wl c h -> p c wl h")
+                lo = 8 * (tile % 4 + j)
+                qv = q_of[tile // 2][:, u : u + 1, c0:c1, :].rearrange("p u c h -> p c u h")
                 if n > 1:
-                    qv = qv.to_broadcast([P, 16, n, 8])
+                    qv = qv.to_broadcast([P, c1 - c0, n, 8])
                 eng.tensor_tensor(
-                    out=pr[:, :, f0 : f0 + w].rearrange("p c (j h) -> p c j h", h=8),
+                    out=prods[k][:, c0:c1, f0 : f0 + w].rearrange("p c (j h) -> p c j h", h=8),
                     in0=qv,
-                    in1=k_rows[hl + i][:, cs, 8 * (wl + j) : 8 * (wl + j) + w].rearrange("p c (j h) -> p c j h", h=8),
+                    in1=k_rows[a][:, c0:c1, lo : lo + w].rearrange("p c (j h) -> p c j h", h=8),
                     op=ALU.mult,
                 )
-            halves[(k, ch)] = pr
+
+        def multiply(k):
+            prods[k] = ring_tile([P, 32, P], F32, "pr")
+            if gpsimd_multiplies(k):
+                products(nc.gpsimd, k, 0, GPSIMD_CHANNELS, q_copies)
+                products(nc.vector, k, GPSIMD_CHANNELS, 32, q_banks)
+            else:
+                products(nc.vector, k, 0, 32, q_banks)
+                halves = prods[k][:].rearrange("p (s c) f -> p s (c f)", s=2)
+                nc.gpsimd.tensor_tensor(out=halves[:, 0], in0=halves[:, 0], in1=halves[:, 1], op=ALU.add)
 
         sts = {}
 
-        def fold(k):
-            a_ap = halves[(k, 0)][:].rearrange("p c f -> p (c f)")
-            nc.gpsimd.tensor_tensor(out=a_ap, in0=a_ap, in1=halves[(k, 1)][:].rearrange("p c f -> p (c f)"), op=ALU.add)
-
         def tensor_reduce(k):
-            parts = (0,) if gpsimd_adds(k) else (1, 0)
+            channels = [c % 32 for c in range(GPSIMD_CHANNELS, GPSIMD_CHANNELS + 32)] if gpsimd_multiplies(k) else list(range(16))
             sts[k] = bank([P, P], F32, "st", "st")
-            for ch in parts:
-                for c in range(16):
-                    nc.tensor.matmul(
-                        out=sts[k][:],
-                        lhsT=halves[(k, ch)][:, c, :],
-                        rhs=ident_f[:],
-                        is_transpose=True,
-                        start=(ch == parts[0] and c == 0),
-                        stop=(ch == parts[-1] and c == 15),
-                    )
+            for c in channels:
+                nc.tensor.matmul(
+                    out=sts[k][:],
+                    lhsT=prods[k][:, c, :],
+                    rhs=ident_f[:],
+                    is_transpose=True,
+                    start=(c == channels[0]),
+                    stop=(c == channels[-1]),
+                )
 
         def copy_st(k):
             stsb = soft.tile([P, P], F32, name="stsb", tag="stsb")
@@ -289,7 +226,9 @@ def tile_relation_kernel(tc, x, w_qkv, out):
                 if tile not in scores:
                     scores[tile] = soft.tile([P, 25, 8], F32, name="sc", tag="sc", bufs=4)
                 a, b = lo - TILE_SCORES * tile, hi - TILE_SCORES * tile
-                nc.scalar.copy(out=scores[tile][:, a // 8 : b // 8, :].rearrange("p o h -> p (o h)"), in_=sts[k][:, lo - P * k : hi - P * k])
+                nc.scalar.copy(
+                    out=scores[tile][:, a // 8 : b // 8, :].rearrange("p o h -> p (o h)"), in_=sts[k][:, lo - P * k : hi - P * k]
+                )
                 lo = hi
 
         minima = {}
@@ -324,14 +263,18 @@ def tile_relation_kernel(tc, x, w_qkv, out):
                 op=ALU.mult,
             )
 
+        def split(tile, o):
+            rows = list(range((o + 4) // 5, 5))
+            return rows, len(rows) * SCALAR_SHARE[tile % len(SCALAR_SHARE)] // 5
+
         def piece_scalar(late, tile, offsets):
-            hl, wl = divmod(tile, 4)
+            wl = tile % 4
             tmp = late.tile([P, 5, 8, 32], F32, name="tmp", tag="tmp", bufs=4)
             for r, o in enumerate(offsets):
                 for h in range(8):
                     nc.scalar.activation(
                         out=tmp[:, r, h, :],
-                        in_=v_rows[hl + o // 5][:, wl + o % 5, h, :],
+                        in_=v_rows[window_row(tile, o // 5)][:, wl + o % 5, h, :],
                         func=ACT.Copy,
                         scale=weights(tile)[:, h, o : o + 1],
                     )
@@ -339,28 +282,27 @@ def tile_relation_kernel(tc, x, w_qkv, out):
 
         psum_weights = {}
 
-        def weights_to_psum(tile):
-            wp = bank([P, 8, 25], F32, "wp", "qa")
-            nc.tensor.matmul(
-                out=wp[:].rearrange("p h o -> p (h o)"),
-                lhsT=ident_f[:],
-                rhs=weights(tile).rearrange("p h o -> p (h o)"),
-                start=True,
-                stop=True,
-            )
-            psum_weights[tile] = wp
+        def weights_to_psum(tile, o):
+            rows, n_scalar = split(tile, o)
+            if n_scalar == len(rows):
+                return
+            lo = 5 * rows[n_scalar]
+            wp = bank([P, 8, 25 - lo], F32, "wp", "qa")
+            nc.tensor.matmul(out=wp[:], lhsT=ident_f[:], rhs=weights(tile)[:, :, lo:25], start=True, stop=True)
+            psum_weights[tile] = (wp, lo)
 
         spare = ["k%d" % r for r in range(8)]
 
         def piece_vector(tile, i):
-            hl, wl = divmod(tile, 4)
+            wl = tile % 4
             tag = spare.pop(0)
             spare.append(tag)
             tmp = keep.tile([P, 5, 8, 32], F32, name="tmv", tag=tag)
+            wp, lo = psum_weights[tile]
             nc.vector.tensor_tensor(
                 out=tmp[:],
-                in0=v_rows[hl + i][:, wl : wl + 5, :, :],
-                in1=psum_weights[tile][:, :, 5 * i : 5 * (i + 1)].rearrange("p h j -> p j h").unsqueeze(3).to_broadcast([P, 5, 8, 32]),
+                in0=v_rows[window_row(tile, i)][:, wl : wl + 5, :, :],
+                in1=wp[:, :, 5 * i - lo : 5 * i - lo + 5].rearrange("p h j -> p j h").unsqueeze(3).to_broadcast([P, 5, 8, 32]),
                 op=ALU.mult,
             )
             return tmp
@@ -372,13 +314,13 @@ def tile_relation_kernel(tc, x, w_qkv, out):
         ots = {}
         done = {}
 
-        def accumulate(late, tile, tmp, n, covers):
+        def accumulate(tile, tmp, n, covers):
             g, wl = divmod(tile, 4)
             if g not in ots:
                 ots[g] = [bank([P, 512], F32, "ot%d" % half, ("w", "qb")[g % 2]) for half in range(2)]
-            first = done.get(tile, 0) == 0
+            opens = tile not in done
             done[tile] = done.get(tile, 0) + covers
-            last = done[tile] == 25
+            closes = done[tile] == 25
             for r in range(n):
                 for half in range(2):
                     nc.tensor.matmul(
@@ -386,46 +328,43 @@ def tile_relation_kernel(tc, x, w_qkv, out):
                         lhsT=tmp[:, r, 4 * half : 4 * (half + 1), :].rearrange("p h c -> p (h c)"),
                         rhs=ident_f[:],
                         is_transpose=True,
-                        start=(first and r == 0),
-                        stop=(last and r == n - 1),
+                        start=(opens and r == 0),
+                        stop=(closes and r == n - 1),
                     )
-            if last and wl == 3:
+            if closes and wl == 3:
                 state["full"].append(g)
 
         def store(late, g):
             for half in range(2):
-                if True:
-                    ost = late.tile([P, 16, 8, 4], F32, name="ost", tag="ost", bufs=2)
-                    src = ots[g][half][:].rearrange("c (wl m wb) -> c m wb wl", wl=4, wb=8)
-                    if half == 0:
-                        nc.vector.tensor_copy(out=ost[:], in_=src)
-                    else:
-                        nc.scalar.copy(out=ost[:], in_=src)
-                    for n_img in range(2):
-                        nc.sync.dma_start(
-                            out=out[n_img, P * half : P * (half + 1)].rearrange("c (hb hl) w -> c hb hl w", hl=4)[:, :, g, :],
-                            in_=ost[:, 8 * n_img : 8 * (n_img + 1)].rearrange("c m wb wl -> c m (wb wl)"),
-                        )
+                ost = late.tile([P, 16, 8, 4], F32, name="ost", tag="ost", bufs=2)
+                src = ots[g][half][:].rearrange("c (wl m wb) -> c m wb wl", wl=4, wb=8)
+                if half == 0:
+                    nc.vector.tensor_copy(out=ost[:], in_=src)
+                else:
+                    nc.scalar.copy(out=ost[:], in_=src)
+                for n in range(2):
+                    nc.sync.dma_start(
+                        out=out[n, P * half : P * (half + 1)].rearrange("c (hb hl) w -> c hb hl w", hl=4)[:, :, ROW_ORDER[g], :],
+                        in_=ost[:, 8 * n : 8 * (n + 1)].rearrange("c m wb wl -> c m (wb wl)"),
+                    )
 
         due = {}
         for tile in range(16):
             due.setdefault(last_chunk(tile) + 4, []).append(tile)
         evacuations = []
-        for name in ("v0", "v1", "v2", "k5", "v3", "v4", "k6", "v5", "k7", "v6", "v7"):
-            evacuations += [(name[0], int(name[1]), b) for b in (0, 2, 4, 6)]
+        for name in ("v2", "v3", "v4", "v5", "v1", "k6", "k7", "v6", "k0", "v7", "v0"):
+            evacuations += [(name[0], int(name[1]), b) for b in (2, 4, 0, 6)]
         state = {"tile": 0, "offset": 0, "ready": -1, "made": [], "full": [], "wp": None}
 
         def step(late, it):
             on = it < N_CHUNKS
             red = 0 <= it - 2 < N_CHUNKS
             bk = 0 <= it - 3 < N_CHUNKS
-            for hl in rows_of(it + 1):
-                if (hl, 0) not in q_banks:
-                    q_bank(hl, 0)
-                    q_copy(hl)
-                    q_bank(hl, 1)
-            for name, a, b0 in evacuations[:EVACUATIONS]:
-                evacuate(name, a, ("w",), (b0,))
+            for pair in pairs_of(it + 1):
+                if pair not in q_banks:
+                    q_bank(pair)
+            for r, (name, a, b0) in enumerate(evacuations[:EVACUATIONS]):
+                evacuate(name, a, (("w", "qb")[r % 2],), (b0,))
             evacuations[:EVACUATIONS] = []
             tile = state["tile"]
             by_tile = not on and tile < 16
@@ -434,40 +373,30 @@ def tile_relation_kernel(tc, x, w_qkv, out):
                 if state["wp"] is None:
                     state["wp"] = tile
                 while state["wp"] <= min(15, tile + 1, state["ready"]):
-                    weights_to_psum(state["wp"])
+                    weights_to_psum(state["wp"], state["offset"] if state["wp"] == tile else 0)
                     state["wp"] += 1
             for m in state["made"]:
-                accumulate(late, *m)
+                accumulate(*m)
             state["made"] = []
             for t in due.get(it, []):
                 softmax_max(t)
             if on:
                 for t in due.get(it - 1, []):
                     softmax_recip(t)
-            if on:
-                if gpsimd_multiplies(it):
-                    products(nc.gpsimd, it, 0, lambda hl: q_copies[hl])
-                else:
-                    products(nc.vector, it, 0, lambda hl: q_banks[(hl, 0)])
-            if on:
+                multiply(it)
                 for t in due.get(it - 1, []):
                     softmax_norm(t)
-                products(nc.vector, it, 1, lambda hl: q_banks[(hl, 1)])
-                if gpsimd_adds(it):
-                    fold(it)
             if bk:
                 back(it - 3)
             if red:
                 tensor_reduce(it - 2)
             if bk:
                 copy_back(it - 3)
-            if not on:
+            if by_tile:
                 for t in due.get(it, []):
                     softmax_exp(t)
-            if by_tile:
                 o = state["offset"]
-                rows = list(range((o + 4) // 5, 5))
-                n_scalar = len(rows) * SCALAR_SHARE[tile % len(SCALAR_SHARE)] // 5
+                rows, n_scalar = split(tile, o)
                 vs = [piece_vector(tile, i) for i in rows[n_scalar:]]
                 for t in due.get(it - 1, []):
                     softmax_recip(t)
@@ -502,27 +431,70 @@ def tile_relation_kernel(tc, x, w_qkv, out):
                 store(late, g)
 
         with tc.tile_pool(name="codes", bufs=1) as codes:
-            every = ("w", "qa", "qb", "st")
-            g2 = gather_row(2)
-            g4 = gather_row(4)
-            quantise_row(codes, 2, g2)
+            side_c = codes.tile([P, 4, 512], U32, name="side_c", align_bytes=64)
+            side_s = codes.tile([P, 4, 512], U8, name="side_s", align_bytes=64)
+            edge_c = codes.tile([P, 4, 1024], U32, name="edge_c", align_bytes=64)
+            edge_s = codes.tile([P, 4, 1024], U8, name="edge_s", align_bytes=64)
+            for side in (side_c[:].bitcast(I32), side_s[:]):
+                side = side.rearrange("p r (m w) -> p r m w", w=8)
+                nc.vector.memset(side[:, :, 0:32, 0:1], 0)
+                nc.vector.memset(side[:, :, 32:64, 7:8], 0)
+            for edge, width, sh in ((edge_c, 64, 8), (edge_s, 16, 2)):
+                edge = edge[:].bitcast(I32).rearrange("p r (m x) -> p r m x", x=width)
+                nc.vector.memset(edge[:, 0:2, :, 0:sh], 0)
+                nc.vector.memset(edge[:, 2:4, :, width - sh : width], 0)
+
+            tiles = {}
+            for a in range(8):
+                for q, b in enumerate((2, 3, 4, 5, 0, 1, 6, 7)):
+                    if a in (0, 1, 6, 7):
+                        c_t, s_t, r, lo = edge_c, edge_s, (0, 1, 6, 7).index(a), P * q
+                    elif q < 4:
+                        c_t, s_t, r, lo = core_c, core_s, a - 2, P * q
+                    else:
+                        c_t, s_t, r, lo = side_c, side_s, a - 2, P * (q - 4)
+                    tiles[(a, b)] = (c_t[:, r, lo : lo + P], s_t[:, r, lo : lo + P])
+
+            wgrp_f = wgrp.bitcast(F32).rearrange("p (w u) -> p w u", u=2)
+            for r in (2, 3, 0, 1, 4, 5):
+                ty, hh = divmod(r, 2)
+                words = wraw[:, r, :].bitcast(F32)
+                wt = bank([P, 2, P], F32, "wt", ("w", "qa", "qb")[ty])
+                for u in range(2):
+                    nc.tensor.transpose(wt[:, u, :], words[:, u:256:2], ident_f[:])
+                if ty < 2:
+                    dst = wgrp_f[:, 256 * ty : 256 * (ty + 1), :].rearrange("p (c h) u -> p c h u", h=8)
+                    dst = dst[:, :, 4 * hh : 4 * (hh + 1), :]
+                    src = wt[:].rearrange("p u (h c) -> p c h u", c=32)
+                else:
+                    dst = wgrp_f[:, 512 + P * hh : 512 + P * (hh + 1), :]
+                    src = wt[:].rearrange("p u r -> p r u")
+                if r % 2 == 0:
+                    nc.vector.tensor_copy(out=dst, in_=src)
+                else:
+                    nc.scalar.copy(out=dst, in_=src)
+
+            gather(0)
+            quantise_w(1)
+            gather(1)
+            quantise(0)
+            quantise_w(0)
+            gather(2)
+            quantise(1)
+            move_columns(0)
+            gather(3)
+            quantise(2)
+            quantise_w(2)
+            quantise(3)
+            move_columns(2)
+            move_rows(True)
+            move_rows(False)
+            every = ("w", "qb", "st")
             evacuate("k", 2, every)
-            g5 = gather_row(5)
-            quantise_row(codes, 4, g4)
-            move_row(codes, 0)
-            evacuate("k", 0, every)
-            g3 = gather_row(3)
-            quantise_row(codes, 5, g5)
-            move_row(codes, 1)
-            evacuate("k", 1, every)
-            quantise_row(codes, 3, g3)
             evacuate("k", 3, every)
-            evacuate("k", 4, every)
-            q_bank(0, 0)
-            q_copy(0)
-            q_bank(0, 1)
-            move_row(codes, 6)
-            move_row(codes, 7)
+            q_bank(0)
+            for a in (4, 5, 1):
+                evacuate("k", a, every)
             it = 0
             while evacuations:
                 step(None, it)

@@ -224,10 +224,10 @@ def tile_relation_kernel(tc, x, w_qkv, out):
                 tile = lo // TILE_SCORES
                 hi = min(P * (k + 1), TILE_SCORES * (tile + 1))
                 if tile not in scores:
-                    scores[tile] = soft.tile([P, 25, 8], F32, name="sc", tag="sc", bufs=4)
-                a, b = lo - TILE_SCORES * tile, hi - TILE_SCORES * tile
+                    scores[tile] = soft.tile([P, 8, 25], F32, name="sc", tag="sc", bufs=4)
+                a, b = (lo - TILE_SCORES * tile) // 8, (hi - TILE_SCORES * tile) // 8
                 nc.scalar.copy(
-                    out=scores[tile][:, a // 8 : b // 8, :].rearrange("p o h -> p (o h)"), in_=sts[k][:, lo - P * k : hi - P * k]
+                    out=scores[tile][:, :, a:b], in_=sts[k][:, lo - P * k : hi - P * k].rearrange("p (o h) -> p h o", h=8)
                 )
                 lo = hi
 
@@ -238,30 +238,30 @@ def tile_relation_kernel(tc, x, w_qkv, out):
 
         def softmax_max(tile):
             mn = soft.tile([P, 8], F32, name="mn", tag="mn")
-            nc.vector.tensor_reduce(out=mn[:], in_=scores[tile][:].rearrange("p o h -> p h o"), axis=AX.X, op=ALU.min)
+            nc.vector.tensor_reduce(out=mn[:], in_=scores[tile][:], axis=AX.X, op=ALU.min)
             minima[tile] = mn
 
         def softmax_exp(tile):
             for h in range(8):
                 nc.scalar.activation(
                     out=weights(tile)[:, h, :],
-                    in_=scores[tile][:, :, h],
+                    in_=scores[tile][:, h, :],
                     func=ACT.Exp,
                     bias=minima[tile][:, h : h + 1],
                     scale=-1.0,
-                    accum_out=sums[:, tile, h : h + 1],
                 )
+
+        def softmax_sum(tile):
+            nc.vector.tensor_reduce(out=sums[:, tile, :], in_=weights(tile), axis=AX.X, op=ALU.add)
 
         def softmax_recip(tile):
             nc.vector.reciprocal(out=sums[:, tile, :], in_=sums[:, tile, :])
 
         def softmax_norm(tile):
-            nc.vector.tensor_tensor(
-                out=weights(tile),
-                in0=weights(tile),
-                in1=sums[:, tile, :].unsqueeze(2).to_broadcast([P, 8, 25]),
-                op=ALU.mult,
-            )
+            for h in range(8):
+                nc.scalar.activation(
+                    out=weights(tile)[:, h, :], in_=weights(tile)[:, h, :], func=ACT.Copy, scale=sums[:, tile, h : h + 1]
+                )
 
         def split(tile, o):
             rows = list(range((o + 4) // 5, 5))
@@ -378,14 +378,13 @@ def tile_relation_kernel(tc, x, w_qkv, out):
             for m in state["made"]:
                 accumulate(*m)
             state["made"] = []
-            for t in due.get(it, []):
-                softmax_max(t)
             if on:
-                for t in due.get(it - 1, []):
-                    softmax_recip(t)
+                for t in due.get(it, []):
+                    softmax_max(t)
                 multiply(it)
                 for t in due.get(it - 1, []):
-                    softmax_norm(t)
+                    softmax_sum(t)
+                    softmax_recip(t)
             if bk:
                 back(it - 3)
             if red:
@@ -393,20 +392,25 @@ def tile_relation_kernel(tc, x, w_qkv, out):
             if bk:
                 copy_back(it - 3)
             if by_tile:
-                for t in due.get(it, []):
-                    softmax_exp(t)
                 o = state["offset"]
                 rows, n_scalar = split(tile, o)
                 vs = [piece_vector(tile, i) for i in rows[n_scalar:]]
                 for t in due.get(it - 1, []):
+                    softmax_sum(t)
+                for t in due.get(it, []):
+                    softmax_max(t)
+                for t in due.get(it - 1, []):
                     softmax_recip(t)
-                    softmax_norm(t)
                 if o % 5:
                     n = 5 - o % 5
                     state["made"].append((tile, piece_scalar(late, tile, list(range(o, o + n))), n, n))
                 for i in rows[:n_scalar]:
-                    state["made"].append((tile, piece_scalar(late, tile, list(range(5 * i, 5 * i + 5))), 5, 5))
-                while len(vs) > 1:
+                    piece = piece_scalar(late, tile, list(range(5 * i, 5 * i + 5)))
+                    if i == 0 and len(vs) % 2 == 1 and tile % 4 == 0:
+                        vs.append(piece)
+                    else:
+                        state["made"].append((tile, piece, 5, 5))
+                while len(vs) > 1 and not (tile == 15 and len(vs) <= 2):
                     add_pieces(vs[0], vs[1])
                     state["made"].append((tile, vs[0], 5, 10))
                     vs = vs[2:]
@@ -423,9 +427,10 @@ def tile_relation_kernel(tc, x, w_qkv, out):
                     state["tile"], state["offset"] = divmod(25 * state["tile"] + o + n, 25)
             if red:
                 copy_st(it - 2)
-            if on:
-                for t in due.get(it, []):
-                    softmax_exp(t)
+            for t in due.get(it - 1, []):
+                softmax_norm(t)
+            for t in due.get(it, []):
+                softmax_exp(t)
             state["ready"] = max([state["ready"]] + due.get(it - 1, []))
             for g in full:
                 store(late, g)

@@ -94,10 +94,13 @@ def tile_relation_kernel(tc, x, w_qkv, out):
         second = ring_tile([P, 8192], BF16, "second")
         third = ring_tile([P, 8192], BF16, "third")
         wraw = first[:, 0:3072].rearrange("p (r k) -> p r k", r=6)
-        nc.sync.dma_start(out=wraw, in_=w_qkv.rearrange("(r p) k -> p r k", p=P))
+        w_rows = w_qkv.rearrange("(r p) k -> p r k", p=P)
         raws = [t[:, 4096:8192].rearrange("p (t m) -> p t m", t=4) for t in (first, second)]
+        nc.sync.dma_start(out=wraw[:, 2:4], in_=w_rows[:, 2:4])
         for n in range(2):
             nc.sync.dma_start(out=raws[n], in_=x[n].rearrange("(p t) h w -> p t (h w)", t=4))
+        nc.sync.dma_start(out=wraw[:, 0:2], in_=w_rows[:, 0:2])
+        nc.sync.dma_start(out=wraw[:, 4:6], in_=w_rows[:, 4:6])
         wgrp = second[:, 0:3072]
         grps = [third[:, 2048 * r : 2048 * (r + 1)] for r in range(4)]
 
@@ -351,7 +354,7 @@ def tile_relation_kernel(tc, x, w_qkv, out):
         due = {}
         for tile in range(16):
             due.setdefault(last_chunk(tile) + 4, []).append(tile)
-        evacuations = []
+        evacuations = [("k", a, 6) for a in (2, 3, 4, 5, 1)]
         for name in ("v2", "v3", "v4", "v5", "v1", "k6", "k7", "v6", "k0", "v7", "v0"):
             evacuations += [(name[0], int(name[1]), b) for b in (2, 4, 0, 6)]
         state = {"tile": 0, "offset": 0, "ready": -1, "made": [], "full": [], "wp": None}
@@ -363,9 +366,10 @@ def tile_relation_kernel(tc, x, w_qkv, out):
             for pair in pairs_of(it + 1):
                 if pair not in q_banks:
                     q_bank(pair)
-            for r, (name, a, b0) in enumerate(evacuations[:EVACUATIONS]):
+            leaving = EVACUATIONS + it % 2
+            for r, (name, a, b0) in enumerate(evacuations[:leaving]):
                 evacuate(name, a, (("w", "qb")[r % 2],), (b0,))
-            evacuations[:EVACUATIONS] = []
+            evacuations[:leaving] = []
             tile = state["tile"]
             by_tile = not on and tile < 16
             full, state["full"] = state["full"], []
@@ -461,48 +465,53 @@ def tile_relation_kernel(tc, x, w_qkv, out):
                     tiles[(a, b)] = (c_t[:, r, lo : lo + P], s_t[:, r, lo : lo + P])
 
             wgrp_f = wgrp.bitcast(F32).rearrange("p (w u) -> p w u", u=2)
-            for r in (2, 3, 0, 1, 4, 5):
-                ty, hh = divmod(r, 2)
-                words = wraw[:, r, :].bitcast(F32)
-                wt = bank([P, 2, P], F32, "wt", ("w", "qa", "qb")[ty])
-                for u in range(2):
-                    nc.tensor.transpose(wt[:, u, :], words[:, u:256:2], ident_f[:])
-                if ty < 2:
-                    dst = wgrp_f[:, 256 * ty : 256 * (ty + 1), :].rearrange("p (c h) u -> p c h u", h=8)
-                    dst = dst[:, :, 4 * hh : 4 * (hh + 1), :]
-                    src = wt[:].rearrange("p u (h c) -> p c h u", c=32)
-                else:
-                    dst = wgrp_f[:, 512 + P * hh : 512 + P * (hh + 1), :]
-                    src = wt[:].rearrange("p u r -> p r u")
-                if r % 2 == 0:
-                    nc.vector.tensor_copy(out=dst, in_=src)
-                else:
-                    nc.scalar.copy(out=dst, in_=src)
+            def regroup_w(ty):
+                for hh in range(2):
+                    r = 2 * ty + hh
+                    words = wraw[:, r, :].bitcast(F32)
+                    wt = bank([P, 2, P], F32, "wt", ("w", "qa", "qb")[ty])
+                    for u in range(2):
+                        nc.tensor.transpose(wt[:, u, :], words[:, u:256:2], ident_f[:])
+                    if ty < 2:
+                        dst = wgrp_f[:, 256 * ty : 256 * (ty + 1), :].rearrange("p (c h) u -> p c h u", h=8)
+                        dst = dst[:, :, 4 * hh : 4 * (hh + 1), :]
+                        src = wt[:].rearrange("p u (h c) -> p c h u", c=32)
+                    else:
+                        dst = wgrp_f[:, 512 + P * hh : 512 + P * (hh + 1), :]
+                        src = wt[:].rearrange("p u r -> p r u")
+                    if hh == 0:
+                        nc.vector.tensor_copy(out=dst, in_=src)
+                    else:
+                        nc.scalar.copy(out=dst, in_=src)
 
-            gather(0)
+            regroup_w(1)
             quantise_w(1)
+            gather(0)
             gather(1)
             quantise(0)
-            quantise_w(0)
             gather(2)
             quantise(1)
-            move_columns(0)
             gather(3)
+            regroup_w(0)
+            move_columns(0)
+            quantise_w(0)
             quantise(2)
-            quantise_w(2)
+            regroup_w(2)
             quantise(3)
+            quantise_w(2)
             move_columns(2)
             move_rows(True)
             move_rows(False)
             every = ("w", "qb", "st")
-            evacuate("k", 2, every)
-            evacuate("k", 3, every)
+            evacuate("k", 2, every, (2, 4, 0))
             q_bank(0)
-            for a in (4, 5, 1):
-                evacuate("k", a, every)
+            for a in (3, 4, 5, 1):
+                evacuate("k", a, every, (2, 4, 0))
             it = 0
             while evacuations:
                 step(None, it)
+                if it == 0:
+                    move_rows(False)
                 it += 1
         with tc.tile_pool(name="late", bufs=4) as late:
             e_parts.append(late.tile([P, 8, 8, 25], F32, name="e_hi", tag="e_hi", bufs=1))

from contextlib import ExitStack

import concourse.mybir as mybir
from concourse.masks import make_identity

F32 = mybir.dt.float32
BF16 = mybir.dt.bfloat16
U32 = mybir.dt.uint32
I32 = mybir.dt.int32
U8 = mybir.dt.uint8
FP8X4 = mybir.dt.float8_e4m3fn_x4
ALU = mybir.AluOpType
ACT = mybir.ActivationFunctionType
AX = mybir.AxisListType

P = 128
FLOPS = 2 * 768 * 512 * 2048 + 2 * 2 * 2048 * 8 * 25 * 32

N_CHUNKS = 25
TILE_SCORES = 200
ROW_ORDER = (1, 2, 3, 0)
GPSIMD_CHANNELS = 12
EVACUATIONS = 5
SCALAR_BUDGET = 6
SCALAR_SHARE = (2, 1)


def window_row(tile, i):
    return ROW_ORDER[tile // 4] + ((i + 1) % 5 if tile < 4 else i)


def segments(k):
    out = []
    u = 16 * k
    while u < 16 * (k + 1):
        tile, o = divmod(u, 25)
        i, j = divmod(o, 5)
        n = min(5 - j, 16 * (k + 1) - u)
        out.append((tile, window_row(tile, i), j, n, 8 * (u - 16 * k)))
        u += n
    return out


def pairs_of(k):
    return sorted(set(s[0] // 2 for s in segments(k))) if 0 <= k < N_CHUNKS else []


def gpsimd_multiplies(k):
    return k % 4 == 0


def last_chunk(tile):
    return (TILE_SCORES * (tile + 1) - 1) // P


def tile_relation_kernel(tc, x, w_qkv, out):
    nc = tc.nc
    with ExitStack() as ctx:
        ctx.enter_context(tc.manual_schedule())
        keep = ctx.enter_context(tc.tile_pool(name="keep", bufs=1))
        ring = ctx.enter_context(tc.tile_pool(name="ring", bufs=3))
        soft = ctx.enter_context(tc.tile_pool(name="soft", bufs=2))
        psum = ctx.enter_context(tc.psum_pool(name="psum", bufs=2))

        ident_f = keep.tile([P, P], F32, name="ident_f")
        make_identity(nc, ident_f[:])
        wc = keep.tile([P, 768], U32, name="wc", align_bytes=64)
        ws = keep.tile([P, 768], U8, name="ws", align_bytes=64)
        k_rows = [keep.tile([P, 32, 64], F32, name="k%d" % r) for r in range(8)]
        v_rows = [keep.tile([P, 8, 8, 32], F32, name="v%d" % r) for r in range(8)]
        core_c = keep.tile([P, 4, 512], U32, name="core_c", align_bytes=64)
        core_s = keep.tile([P, 4, 512], U8, name="core_s", align_bytes=64)
        e_parts = [keep.tile([P, 8, 8, 25], F32, name="e_lo")]
        sums = keep.tile([P, 16, 8], F32, name="sums")

        def bank(shape, dtype, name, tag):
            return psum.tile(shape, dtype, name=name, tag=tag, bufs=2)

        def ring_tile(shape, dtype, name):
            return ring.tile(shape, dtype, name=name, tag="b16", align_bytes=64)

        def project(dst, codes, scales, lo, hi):
            nc.tensor.matmul_mx(
                out=dst,
                lhsT=codes.bitcast(FP8X4),
                lhsT_scale=scales,
                rhs=wc[:, lo:hi].bitcast(FP8X4),
                rhs_scale=ws[:, lo:hi],
                start=True,
                stop=True,
            )

        first = ring_tile([P, 8192], BF16, "first")
        second = ring_tile([P, 8192], BF16, "second")
        third = ring_tile([P, 8192], BF16, "third")
        wraw = first[:, 0:3072].rearrange("p (r k) -> p r k", r=6)
        w_rows = w_qkv.rearrange("(r p) k -> p r k", p=P)
        raws = [t[:, 4096:8192].rearrange("p (t m) -> p t m", t=4) for t in (first, second)]
        nc.sync.dma_start(out=wraw[:, 2:4], in_=w_rows[:, 2:4])
        for n in range(2):
            nc.sync.dma_start(out=raws[n], in_=x[n].rearrange("(p t) h w -> p t (h w)", t=4))
        nc.sync.dma_start(out=wraw[:, 0:2], in_=w_rows[:, 0:2])
        nc.sync.dma_start(out=wraw[:, 4:6], in_=w_rows[:, 4:6])
        wgrp = second[:, 0:3072]
        grps = [third[:, 2048 * r : 2048 * (r + 1)] for r in range(4)]

        def gather(r):
            dst = grps[r].rearrange("p (c n h w t) -> p c n h w t", c=4, n=2, h=8, w=8)
            for n, eng, c0, c1 in ((0, nc.vector.tensor_copy, 0, 4), (1, nc.scalar.copy, 2, 4), (1, nc.vector.tensor_copy, 0, 2)):
                src = raws[n].rearrange("p t (h r w c) -> p r c h w t", h=8, r=4, w=8)
                eng(out=dst[:, c0:c1, n], in_=src[:, r, c0:c1])

        def quantise(r):
            nc.vector.quantize_mx(out=core_c[:, r, :].bitcast(FP8X4), scales=core_s[:, r, :], in_=grps[r])

        def quantise_w(ty):
            cols = slice(256 * ty, 256 * (ty + 1))
            nc.vector.quantize_mx(out=wc[:, cols].bitcast(FP8X4), scales=ws[:, cols], in_=wgrp[:, 1024 * ty : 1024 * (ty + 1)])

        def move_columns(r0):
            for dst_t, src_t in ((side_c, core_c), (side_s, core_s)):
                dst, src = dst_t[:, r0 : r0 + 2, :], src_t[:, r0 : r0 + 2, :]
                if dst_t is side_c:
                    dst, src = dst.bitcast(I32), src.bitcast(I32)
                dst = dst.rearrange("p r (m w) -> p r m w", w=8)
                src = src.rearrange("p r (m w) -> p r m w", w=8)
                nc.vector.tensor_copy(out=dst[:, :, 0:32, 1:8], in_=src[:, :, 32:64, 0:7])
                nc.vector.tensor_copy(out=dst[:, :, 32:64, 0:7], in_=src[:, :, 0:32, 1:8])

        def move_rows(up):
            d0, r0 = (0, 2) if up else (2, 0)
            for dst_t, core_t, side_t, width, sh in ((edge_c, core_c, side_c, 64, 8), (edge_s, core_s, side_s, 16, 2)):
                for half, src_t in enumerate((core_t, side_t)):
                    dst = dst_t[:, d0 : d0 + 2, 512 * half : 512 * (half + 1)].bitcast(I32)
                    dst = dst.rearrange("p r (m x) -> p r m x", x=width)
                    src = src_t[:, r0 : r0 + 2, :].bitcast(I32).rearrange("p r (m x) -> p r m x", x=width)
                    if up:
                        nc.vector.tensor_copy(out=dst[:, :, :, sh:width], in_=src[:, :, :, 0 : width - sh])
                    else:
                        nc.vector.tensor_copy(out=dst[:, :, :, 0 : width - sh], in_=src[:, :, :, sh:width])

        def evacuate(what, a, tags, pairs=(2, 4, 0, 6)):
            for r, b0 in enumerate(pairs):
                ps = bank([P, 2, 256], F32, "ps", tags[r % len(tags)])
                for u in range(2):
                    lo = 256 if what == "k" else 512
                    project(ps[:, u, :], tiles[(a, b0 + u)][0], tiles[(a, b0 + u)][1], lo, lo + 256)
                if what == "k":
                    nc.scalar.copy(
                        out=k_rows[a][:, :, 8 * b0 : 8 * (b0 + 2)].rearrange("p c (u h) -> p c u h", h=8),
                        in_=ps[:].rearrange("p u (c h) -> p c u h", h=8),
                    )
                else:
                    nc.scalar.copy(out=v_rows[a][:, b0 : b0 + 2, :, :].rearrange("p b h c -> p b (h c)"), in_=ps[:])

        q_banks = {}
        q_copies = {}

        def q_bank(pair):
            g, w0 = divmod(2 * pair, 4)
            qp = bank([P, 2, 32, 8], F32, "qp", "qa")
            for u in range(2):
                codes_q, scales_q = tiles[(ROW_ORDER[g] + 2, w0 + u + 2)]
                project(qp[:, u, :, :].rearrange("p c h -> p (c h)"), codes_q, scales_q, 0, 256)
            qs = soft.tile([P, 2, GPSIMD_CHANNELS, 8], F32, name="qs", tag="qs")
            nc.scalar.copy(out=qs[:], in_=qp[:, :, 0:GPSIMD_CHANNELS, :])
            q_banks[pair] = qp
            q_copies[pair] = qs

        prods = {}

        def products(eng, k, c0, c1, q_of):
            for tile, a, j, n, f0 in segments(k):
                u = tile % 2
                w = 8 * n
                lo = 8 * (tile % 4 + j)
                qv = q_of[tile // 2][:, u : u + 1, c0:c1, :].rearrange("p u c h -> p c u h")
                if n > 1:
                    qv = qv.to_broadcast([P, c1 - c0, n, 8])
                eng.tensor_tensor(
                    out=prods[k][:, c0:c1, f0 : f0 + w].rearrange("p c (j h) -> p c j h", h=8),
                    in0=qv,
                    in1=k_rows[a][:, c0:c1, lo : lo + w].rearrange("p c (j h) -> p c j h", h=8),
                    op=ALU.mult,
                )

        def multiply(k):
            prods[k] = ring_tile([P, 32, P], F32, "pr")
            if gpsimd_multiplies(k):
                products(nc.gpsimd, k, 0, GPSIMD_CHANNELS, q_copies)
                products(nc.vector, k, GPSIMD_CHANNELS, 32, q_banks)
            else:
                products(nc.vector, k, 0, 32, q_banks)
                halves = prods[k][:].rearrange("p (s c) f -> p s (c f)", s=2)
                nc.gpsimd.tensor_tensor(out=halves[:, 0], in0=halves[:, 0], in1=halves[:, 1], op=ALU.add)

        sts = {}

        def tensor_reduce(k):
            channels = [c % 32 for c in range(GPSIMD_CHANNELS, GPSIMD_CHANNELS + 32)] if gpsimd_multiplies(k) else list(range(16))
            sts[k] = bank([P, P], F32, "st", "st")
            for c in channels:
                nc.tensor.matmul(
                    out=sts[k][:],
                    lhsT=prods[k][:, c, :],
                    rhs=ident_f[:],
                    is_transpose=True,
                    start=(c == channels[0]),
                    stop=(c == channels[-1]),
                )

        def copy_st(k):
            stsb = soft.tile([P, P], F32, name="stsb", tag="stsb")
            nc.scalar.activation(out=stsb[:], in_=sts[k][:], func=ACT.Copy, scale=-1.0)
            sts[k] = stsb

        def back(k):
            sbp = bank([P, P], F32, "sbp", "st")
            nc.tensor.transpose(sbp[:], sts[k][:], ident_f[:])
            sts[k] = sbp

        scores = {}

        def copy_back(k):
            lo = P * k
            while lo < P * (k + 1):
                tile = lo // TILE_SCORES
                hi = min(P * (k + 1), TILE_SCORES * (tile + 1))
                if tile not in scores:
                    scores[tile] = soft.tile([P, 8, 25], F32, name="sc", tag="sc", bufs=4)
                a, b = (lo - TILE_SCORES * tile) // 8, (hi - TILE_SCORES * tile) // 8
                nc.scalar.copy(
                    out=scores[tile][:, :, a:b], in_=sts[k][:, lo - P * k : hi - P * k].rearrange("p (o h) -> p h o", h=8)
                )
                lo = hi

        minima = {}

        def weights(tile):
            return e_parts[tile // 8][:, tile % 8, :, :]

        def softmax_max(tile):
            mn = soft.tile([P, 8], F32, name="mn", tag="mn")
            nc.vector.tensor_reduce(out=mn[:], in_=scores[tile][:], axis=AX.X, op=ALU.min)
            minima[tile] = mn

        def softmax_exp(tile):
            for h in range(8):
                nc.scalar.activation(
                    out=weights(tile)[:, h, :],
                    in_=scores[tile][:, h, :],
                    func=ACT.Exp,
                    bias=minima[tile][:, h : h + 1],
                    scale=-1.0,
                )

        def softmax_sum(tile):
            nc.vector.tensor_reduce(out=sums[:, tile, :], in_=weights(tile), axis=AX.X, op=ALU.add)

        def softmax_recip(tile):
            nc.vector.reciprocal(out=sums[:, tile, :], in_=sums[:, tile, :])

        def softmax_norm(tile):
            for h in range(8):
                nc.scalar.activation(
                    out=weights(tile)[:, h, :], in_=weights(tile)[:, h, :], func=ACT.Copy, scale=sums[:, tile, h : h + 1]
                )

        def split(tile, o):
            rows = list(range((o + 4) // 5, 5))
            return rows, len(rows) * SCALAR_SHARE[tile % len(SCALAR_SHARE)] // 5

        def piece_scalar(late, tile, offsets):
            wl = tile % 4
            tmp = late.tile([P, 5, 8, 32], F32, name="tmp", tag="tmp", bufs=4)
            for r, o in enumerate(offsets):
                for h in range(8):
                    nc.scalar.activation(
                        out=tmp[:, r, h, :],
                        in_=v_rows[window_row(tile, o // 5)][:, wl + o % 5, h, :],
                        func=ACT.Copy,
                        scale=weights(tile)[:, h, o : o + 1],
                    )
            return tmp

        psum_weights = {}

        def weights_to_psum(tile, o):
            rows, n_scalar = split(tile, o)
            if n_scalar == len(rows):
                return
            lo = 5 * rows[n_scalar]
            wp = bank([P, 8, 25 - lo], F32, "wp", "qa")
            nc.tensor.matmul(out=wp[:], lhsT=ident_f[:], rhs=weights(tile)[:, :, lo:25], start=True, stop=True)
            psum_weights[tile] = (wp, lo)

        spare = ["k%d" % r for r in range(8)]

        def piece_vector(tile, i):
            wl = tile % 4
            tag = spare.pop(0)
            spare.append(tag)
            tmp = keep.tile([P, 5, 8, 32], F32, name="tmv", tag=tag)
            wp, lo = psum_weights[tile]
            nc.vector.tensor_tensor(
                out=tmp[:],
                in0=v_rows[window_row(tile, i)][:, wl : wl + 5, :, :],
                in1=wp[:, :, 5 * i - lo : 5 * i - lo + 5].rearrange("p h j -> p j h").unsqueeze(3).to_broadcast([P, 5, 8, 32]),
                op=ALU.mult,
            )
            return tmp

        def add_pieces(t0, t1):
            a_ap = t0[:].rearrange("p j h c -> p (j h c)")
            nc.gpsimd.tensor_tensor(out=a_ap, in0=a_ap, in1=t1[:].rearrange("p j h c -> p (j h c)"), op=ALU.add)

        ots = {}
        done = {}

        def accumulate(tile, tmp, n, covers):
            g, wl = divmod(tile, 4)
            if g not in ots:
                ots[g] = [bank([P, 512], F32, "ot%d" % half, ("w", "qb")[g % 2]) for half in range(2)]
            opens = tile not in done
            done[tile] = done.get(tile, 0) + covers
            closes = done[tile] == 25
            for r in range(n):
                for half in range(2):
                    nc.tensor.matmul(
                        out=ots[g][half][:, P * wl : P * (wl + 1)],
                        lhsT=tmp[:, r, 4 * half : 4 * (half + 1), :].rearrange("p h c -> p (h c)"),
                        rhs=ident_f[:],
                        is_transpose=True,
                        start=(opens and r == 0),
                        stop=(closes and r == n - 1),
                    )
            if closes and wl == 3:
                state["full"].append(g)

        def store(late, g):
            for half in range(2):
                ost = late.tile([P, 16, 8, 4], F32, name="ost", tag="ost", bufs=2)
                src = ots[g][half][:].rearrange("c (wl m wb) -> c m wb wl", wl=4, wb=8)
                if half == 0:
                    nc.vector.tensor_copy(out=ost[:], in_=src)
                else:
                    nc.scalar.copy(out=ost[:], in_=src)
                for n in range(2):
                    nc.sync.dma_start(
                        out=out[n, P * half : P * (half + 1)].rearrange("c (hb hl) w -> c hb hl w", hl=4)[:, :, ROW_ORDER[g], :],
                        in_=ost[:, 8 * n : 8 * (n + 1)].rearrange("c m wb wl -> c m (wb wl)"),
                    )

        due = {}
        for tile in range(16):
            due.setdefault(last_chunk(tile) + 4, []).append(tile)
        evacuations = [("k", a, 6) for a in (2, 3, 4, 5, 1)]
        for name in ("v2", "v3", "v4", "v5", "v1", "k6", "k7", "v6", "k0", "v7", "v0"):
            evacuations += [(name[0], int(name[1]), b) for b in (2, 4, 0, 6)]
        state = {"tile": 0, "offset": 0, "ready": -1, "made": [], "full": [], "wp": None}

        def step(late, it):
            on = it < N_CHUNKS
            red = 0 <= it - 2 < N_CHUNKS
            bk = 0 <= it - 3 < N_CHUNKS
            for pair in pairs_of(it + 1):
                if pair not in q_banks:
                    q_bank(pair)
            leaving = EVACUATIONS + it % 2
            for r, (name, a, b0) in enumerate(evacuations[:leaving]):
                evacuate(name, a, (("w", "qb")[r % 2],), (b0,))
            evacuations[:leaving] = []
            tile = state["tile"]
            by_tile = not on and tile < 16
            full, state["full"] = state["full"], []
            if by_tile:
                if state["wp"] is None:
                    state["wp"] = tile
                while state["wp"] <= min(15, tile + 1, state["ready"]):
                    weights_to_psum(state["wp"], state["offset"] if state["wp"] == tile else 0)
                    state["wp"] += 1
            for m in state["made"]:
                accumulate(*m)
            state["made"] = []
            if on:
                for t in due.get(it, []):
                    softmax_max(t)
                multiply(it)
                for t in due.get(it - 1, []):
                    softmax_sum(t)
                    softmax_recip(t)
            if bk:
                back(it - 3)
            if red:
                tensor_reduce(it - 2)
            if bk:
                copy_back(it - 3)
            if by_tile:
                o = state["offset"]
                rows, n_scalar = split(tile, o)
                vs = [piece_vector(tile, i) for i in rows[n_scalar:]]
                for t in due.get(it - 1, []):
                    softmax_sum(t)
                for t in due.get(it, []):
                    softmax_max(t)
                for t in due.get(it - 1, []):
                    softmax_recip(t)
                if o % 5:
                    n = 5 - o % 5
                    state["made"].append((tile, piece_scalar(late, tile, list(range(o, o + n))), n, n))
                for i in rows[:n_scalar]:
                    piece = piece_scalar(late, tile, list(range(5 * i, 5 * i + 5)))
                    if i == 0 and len(vs) % 2 == 1 and tile % 4 == 0:
                        vs.append(piece)
                    else:
                        state["made"].append((tile, piece, 5, 5))
                while len(vs) > 1 and not (tile == 15 and len(vs) <= 2):
                    add_pieces(vs[0], vs[1])
                    state["made"].append((tile, vs[0], 5, 10))
                    vs = vs[2:]
                for v in vs:
                    state["made"].append((tile, v, 5, 5))
                state["tile"], state["offset"] = tile + 1, 0
            elif on and late is not None:
                budget = SCALAR_BUDGET
                while budget > 0 and state["tile"] <= state["ready"]:
                    o = state["offset"]
                    n = min(5 - o % 5, budget)
                    state["made"].append((state["tile"], piece_scalar(late, state["tile"], list(range(o, o + n))), n, n))
                    budget -= n
                    state["tile"], state["offset"] = divmod(25 * state["tile"] + o + n, 25)
            if red:
                copy_st(it - 2)
            for t in due.get(it - 1, []):
                softmax_norm(t)
            for t in due.get(it, []):
                softmax_exp(t)
            state["ready"] = max([state["ready"]] + due.get(it - 1, []))
            for g in full:
                store(late, g)

        with tc.tile_pool(name="codes", bufs=1) as codes:
            side_c = codes.tile([P, 4, 512], U32, name="side_c", align_bytes=64)
            side_s = codes.tile([P, 4, 512], U8, name="side_s", align_bytes=64)
            edge_c = codes.tile([P, 4, 1024], U32, name="edge_c", align_bytes=64)
            edge_s = codes.tile([P, 4, 1024], U8, name="edge_s", align_bytes=64)
            for side in (side_c[:].bitcast(I32), side_s[:]):
                side = side.rearrange("p r (m w) -> p r m w", w=8)
                nc.vector.memset(side[:, :, 0:32, 0:1], 0)
                nc.vector.memset(side[:, :, 32:64, 7:8], 0)
            for edge, width, sh in ((edge_c, 64, 8), (edge_s, 16, 2)):
                edge = edge[:].bitcast(I32).rearrange("p r (m x) -> p r m x", x=width)
                nc.vector.memset(edge[:, 0:2, :, 0:sh], 0)
                nc.vector.memset(edge[:, 2:4, :, width - sh : width], 0)

            tiles = {}
            for a in range(8):
                for q, b in enumerate((2, 3, 4, 5, 0, 1, 6, 7)):
                    if a in (0, 1, 6, 7):
                        c_t, s_t, r, lo = edge_c, edge_s, (0, 1, 6, 7).index(a), P * q
                    elif q < 4:
                        c_t, s_t, r, lo = core_c, core_s, a - 2, P * q
                    else:
                        c_t, s_t, r, lo = side_c, side_s, a - 2, P * (q - 4)
                    tiles[(a, b)] = (c_t[:, r, lo : lo + P], s_t[:, r, lo : lo + P])

            wgrp_f = wgrp.bitcast(F32).rearrange("p (w u) -> p w u", u=2)
            def regroup_w(ty):
                for hh in range(2):
                    r = 2 * ty + hh
                    words = wraw[:, r, :].bitcast(F32)
                    wt = bank([P, 2, P], F32, "wt", ("w", "qa", "qb")[ty])
                    for u in range(2):
                        nc.tensor.transpose(wt[:, u, :], words[:, u:256:2], ident_f[:])
                    if ty < 2:
                        dst = wgrp_f[:, 256 * ty : 256 * (ty + 1), :].rearrange("p (c h) u -> p c h u", h=8)
                        dst = dst[:, :, 4 * hh : 4 * (hh + 1), :]
                        src = wt[:].rearrange("p u (h c) -> p c h u", c=32)
                    else:
                        dst = wgrp_f[:, 512 + P * hh : 512 + P * (hh + 1), :]
                        src = wt[:].rearrange("p u r -> p r u")
                    if hh == 0:
                        nc.vector.tensor_copy(out=dst, in_=src)
                    else:
                        nc.scalar.copy(out=dst, in_=src)

            regroup_w(1)
            quantise_w(1)
            gather(0)
            gather(1)
            quantise(0)
            gather(2)
            quantise(1)
            gather(3)
            regroup_w(0)
            move_columns(0)
            quantise_w(0)
            quantise(2)
            regroup_w(2)
            quantise(3)
            quantise_w(2)
            move_columns(2)
            move_rows(True)
            move_rows(False)
            every = ("w", "qb", "st")
            evacuate("k", 2, every, (2, 4, 0))
            q_bank(0)
            for a in (3, 4, 5, 1):
                evacuate("k", a, every, (2, 4, 0))
            it = 0
            while evacuations:
                step(None, it)
                if it == 0:
                    move_rows(False)
                it += 1
        with tc.tile_pool(name="late", bufs=4) as late:
            e_parts.append(late.tile([P, 8, 8, 25], F32, name="e_hi", tag="e_hi", bufs=1))
            while it < N_CHUNKS or state["tile"] < 16 or state["made"] or state["full"]:
                step(late, it)
                it += 1
